import numpy as np
import ml_dtypes


def mxq(x, axis, fmt="e4m3"):
    dtype, down = {"e4m3": (ml_dtypes.float8_e4m3fn, 7), "e5m2": (ml_dtypes.float8_e5m2, 14)}[fmt]
    v = np.moveaxis(np.asarray(x, np.float32).astype(ml_dtypes.bfloat16).astype(np.float64), axis, -1)
    blocks = v.reshape(v.shape[:-1] + (-1, 32))
    amax = np.abs(blocks).max(-1, keepdims=True)
    byte = np.maximum(np.where(amax > 0, np.frexp(amax)[1] - 1 + 127, 0) - down, 1)
    scale = np.exp2(byte - 127.0)
    codes = (blocks / scale).astype(np.float32).astype(dtype).astype(np.float64)
    return np.moveaxis((codes * scale).reshape(v.shape), -1, axis)


WIDE = False


def mx_kscale(k):
    if not WIDE:
        return np.ones(k)
    levels = np.array([10, -10, 5, -5, 0])
    a = np.random.permutation(np.resize(levels, k // 512 * 4)).reshape(k // 512, 4)
    idx = np.arange(k)
    return np.exp2(a[idx // 512, idx % 128 // 32])


BF16 = ml_dtypes.bfloat16


def bf(x):
    return np.asarray(x, np.float32).astype(BF16)


def f64(x):
    return np.asarray(x).astype(np.float64)


B, STOCH, ACT_DIM, HIDDEN, DETER = 256, 1024, 512, 2048, 2048
K1 = STOCH + ACT_DIM
EPS = 1e-4


def silu(v):
    return v / (1.0 + np.exp(-v))


def rmsnorm(v, w):
    return v * (1.0 / np.sqrt(np.mean(v * v, axis=-1, keepdims=True) + EPS)) * w


def setup_inputs():
    s = mx_kscale(K1)[:STOCH]
    w1 = np.random.standard_normal((HIDDEN, K1)) * 0.07 / np.sqrt(K1)
    w1[:, :STOCH] = w1[:, :STOCH] / s
    return {"stoch": bf(np.random.standard_normal((B, STOCH)) * s),
            "action": bf(np.random.standard_normal((B, ACT_DIM))),
            "tok_w1": bf(w1),
            "tok_b1": bf(np.random.standard_normal(HIDDEN) * 0.03),
            "tok_nw": bf(1.0 + 0.1 * np.random.standard_normal(HIDDEN)),
            "tok_w2": bf(np.random.standard_normal((DETER, HIDDEN)) * 1.5 / np.sqrt(HIDDEN)),
            "tok_b2": bf(np.random.standard_normal(DETER) * 0.2)}


def reference(stoch, action, tok_w1, tok_b1, tok_nw, tok_w2, tok_b2):
    act = f64(action)
    act = act / np.maximum(np.abs(act), 1.0)
    u = np.concatenate([f64(stoch), act], axis=-1)
    h = (mxq(u, 1, "e4m3") @ mxq(f64(tok_w1), 1, "e4m3").T) + f64(tok_b1)
    g = silu(rmsnorm(h, f64(tok_nw)))
    return (mxq(g, 1, "e4m3") @ mxq(f64(tok_w2), 1, "e4m3").T) + f64(tok_b2)

@@ -1,0 +1,278 @@
+from contextlib import ExitStack
+
+import concourse.mybir as mybir
+from concourse.masks import make_identity
+
+F32 = mybir.dt.float32
+BF16 = mybir.dt.bfloat16
+U32 = mybir.dt.uint32
+U8 = mybir.dt.uint8
+FP8X4 = mybir.dt.float8_e4m3fn_x4
+ALU = mybir.AluOpType
+ACT = mybir.ActivationFunctionType
+AXIS = mybir.AxisListType
+
+P = 128
+PACK = 4
+K_PASS = P * PACK
+WORDS_PER_PASS = K_PASS // 2
+
+TOKENS, STOCH, ACT_DIM, HIDDEN, DETER = 256, 1024, 512, 2048, 2048
+K1 = STOCH + ACT_DIM
+EPS = 1e-4
+TOKEN_TILES = TOKENS // P
+
+CHUNK = 512
+ROWS_PER_PARTITION = CHUNK // P
+CHUNKS = HIDDEN // CHUNK
+PASSES_1 = K1 // K_PASS
+PASSES_2 = HIDDEN // K_PASS
+RAW_BUFS = 4
+
+FLOPS = 2 * TOKENS * (K1 * HIDDEN + HIDDEN * DETER)
+
+
+def tile_mamba2backbone_pa_kernel(
+    tc, stoch, action, tok_w1, tok_b1, tok_nw, tok_w2, tok_b2, out
+):
+    nc = tc.nc
+    with ExitStack() as ctx:
+        keep = ctx.enter_context(tc.tile_pool(name="keep", bufs=1))
+        raw_pool = ctx.enter_context(tc.tile_pool(name="raw", bufs=RAW_BUFS))
+        stage = ctx.enter_context(tc.tile_pool(name="stage", bufs=4))
+        biased = ctx.enter_context(tc.tile_pool(name="biased", bufs=6))
+        unread = ctx.enter_context(tc.tile_pool(name="unread", bufs=2))
+        result = ctx.enter_context(tc.tile_pool(name="result", bufs=2))
+        psum_t = ctx.enter_context(tc.psum_pool(name="psum_t", bufs=6))
+        psum_acc = ctx.enter_context(tc.psum_pool(name="psum_acc", bufs=2))
+        ctx.enter_context(tc.manual_schedule())
+
+        ident = keep.tile([P, P], F32)
+        ident_bf = keep.tile([P, P], BF16)
+        vec_rows = keep.tile([P, HIDDEN], BF16)
+        b1_all = keep.tile([P, HIDDEN], BF16)
+        nw_all = keep.tile([P, HIDDEN], BF16)
+        b2_all = keep.tile([P, DETER], BF16)
+        u_sb = keep.tile([P, TOKEN_TILES * K1], BF16)
+        u_codes = keep.tile([P, PASSES_1, TOKENS], U32, align_bytes=64)
+        u_scales = keep.tile([P, PASSES_1, TOKENS], U8, align_bytes=64)
+        w1_codes = keep.tile([P, CHUNKS, PASSES_1, CHUNK], U32, align_bytes=64)
+        w1_scales = keep.tile([P, CHUNKS, PASSES_1, CHUNK], U8, align_bytes=64)
+        w2_codes = keep.tile([P, CHUNKS, PASSES_2, CHUNK], U32, align_bytes=64)
+        w2_scales = keep.tile([P, CHUNKS, PASSES_2, CHUNK], U8, align_bytes=64)
+        gained = keep.tile([P, TOKEN_TILES, HIDDEN], F32)
+        g_sb = keep.tile([P, TOKEN_TILES * HIDDEN], BF16)
+        g_codes = keep.tile([P, PASSES_2, TOKENS], U32, align_bytes=64)
+        g_scales = keep.tile([P, PASSES_2, TOKENS], U8, align_bytes=64)
+        square_sums = keep.tile([P, TOKEN_TILES, CHUNKS], F32)
+        row_sum = keep.tile([P, TOKEN_TILES], F32)
+        mean_eps = keep.tile([P, TOKEN_TILES], F32)
+        minus_half = keep.tile([P, TOKEN_TILES], F32)
+        rstd = keep.tile([P, TOKEN_TILES], F32)
+        table_warmer = keep.tile([P, TOKEN_TILES], F32)
+
+        def load_chunk(weight, i):
+            k = weight.shape[1]
+            raw = raw_pool.tile([P, ROWS_PER_PARTITION * k], BF16, tag="raw")
+            rows = weight[CHUNK * i : CHUNK * (i + 1), :]
+            nc.sync.dma_start(
+                out=raw[:], in_=rows.rearrange("(j e) k -> j (e k)", e=ROWS_PER_PARTITION)
+            )
+            return raw
+
+        def quantise_pass(source, k, blocks, c, codes, scales, copies):
+            words = source[:].bitcast(F32)
+            grouped = stage.tile([P, blocks * P * PACK], BF16, tag="grouped", align_bytes=64)
+            grouped_words = grouped[:].bitcast(F32).rearrange(
+                "p (b r h) -> p b r h", b=blocks, h=2
+            )
+            for pair in range(blocks // 2):
+                bank = psum_t.tile([P, 2, 2, P], F32, tag="bank")
+                for b in range(2):
+                    for h in range(2):
+                        first = (2 * pair + b) * (k // 2) + WORDS_PER_PASS * c + P * h
+                        nc.tensor.transpose(
+                            bank[:, b, h, :], words[:, first : first + P], ident[:]
+                        )
+                copies[pair](
+                    out=grouped_words[:, 2 * pair : 2 * pair + 2],
+                    in_=bank[:].rearrange("p b h r -> p b r h"),
+                )
+            nc.vector.quantize_mx(out=codes.bitcast(FP8X4), scales=scales, in_=grouped[:])
+
+        def quantise_chunk_pass(raw, k, c, codes, scales, copies):
+            quantise_pass(raw, k, ROWS_PER_PARTITION, c, codes[:, c, :], scales[:, c, :], copies)
+
+        def quantise_w1_chunk(i):
+            for c in range(PASSES_1):
+                quantise_chunk_pass(
+                    raw_w1[i], K1, c, w1_codes[:, i, :, :], w1_scales[:, i, :, :], by_scalar
+                )
+
+        def quantise_w2_chunk(i):
+            for c in range(PASSES_2):
+                quantise_chunk_pass(
+                    raw_w2[i], HIDDEN, c, w2_codes[:, i, :, :], w2_scales[:, i, :, :], by_scalar
+                )
+
+        def spread_row(row, everywhere):
+            pick = ident_bf[:, row : row + 1].to_broadcast([P, P])
+            for half in range(2):
+                row_bank = psum_t.tile([P, 2 * CHUNK], BF16, tag="bank")
+                for quarter in range(2):
+                    first = 2 * CHUNK * half + CHUNK * quarter
+                    nc.tensor.matmul(
+                        out=row_bank[:, CHUNK * quarter : CHUNK * (quarter + 1)],
+                        lhsT=pick,
+                        rhs=vec_rows[:, first : first + CHUNK],
+                        start=True,
+                        stop=True,
+                    )
+                nc.scalar.copy(
+                    out=everywhere[:, 2 * CHUNK * half : 2 * CHUNK * (half + 1)], in_=row_bank[:]
+                )
+
+        def products(acts_codes, acts_scales, codes, scales, passes, t):
+            acc = psum_acc.tile([P, CHUNK], F32, tag="acc")
+            tokens = slice(P * t, P * (t + 1))
+            for c in range(passes):
+                nc.tensor.matmul_mx(
+                    out=acc[:],
+                    lhsT=acts_codes[:, c, tokens].bitcast(FP8X4),
+                    lhsT_scale=acts_scales[:, c, tokens],
+                    rhs=codes[:, c, :].bitcast(FP8X4),
+                    rhs_scale=scales[:, c, :],
+                    start=(c == 0),
+                    stop=(c == passes - 1),
+                )
+            return acc
+
+        def add_bias(dest, acc, bias):
+            nc.vector.tensor_tensor(
+                out=dest.rearrange("p (j e) -> p j e", e=ROWS_PER_PARTITION),
+                in0=acc[:].rearrange("p (e j) -> p j e", e=ROWS_PER_PARTITION),
+                in1=bias.rearrange("p (j e) -> p j e", e=ROWS_PER_PARTITION),
+                op=ALU.add,
+            )
+
+        def layer1_products(i):
+            for t in range(TOKEN_TILES):
+                acc = products(u_codes, u_scales, w1_codes[:, i, :, :], w1_scales[:, i, :, :], PASSES_1, t)
+                h_biased = biased.tile([P, CHUNK], F32, tag="h_biased")
+                add_bias(h_biased[:], acc, b1_all[:, CHUNK * i : CHUNK * (i + 1)])
+                h_tiles[(i, t)] = h_biased
+
+        def layer1_statistics(i):
+            columns = slice(CHUNK * i, CHUNK * (i + 1))
+            for t in range(TOKEN_TILES):
+                squares = unread.tile([P, CHUNK], BF16, tag="squares")
+                nc.scalar.activation(
+                    out=squares[:],
+                    in_=h_tiles[(i, t)][:],
+                    func=ACT.Square,
+                    accum_out=square_sums[:, t, i : i + 1],
+                )
+                nc.vector.tensor_tensor(
+                    out=gained[:, t, columns],
+                    in0=h_tiles[(i, t)][:],
+                    in1=nw_all[:, columns],
+                    op=ALU.mult,
+                )
+
+        def layer2_products(i):
+            columns = slice(CHUNK * i, CHUNK * (i + 1))
+            out_sb = result.tile([P, TOKEN_TILES, CHUNK], F32, tag="out_sb")
+            for t in range(TOKEN_TILES):
+                acc = products(g_codes, g_scales, w2_codes[:, i, :, :], w2_scales[:, i, :, :], PASSES_2, t)
+                add_bias(out_sb[:, t, :], acc, b2_all[:, columns])
+            nc.sync.dma_start(
+                out=out.rearrange("(p t) n -> p t n", t=TOKEN_TILES)[:, :, columns], in_=out_sb[:]
+            )
+
+        by_scalar = (nc.scalar.copy, nc.scalar.copy)
+        by_both = (nc.scalar.copy, nc.vector.tensor_copy)
+        by_vector = (nc.vector.tensor_copy,)
+        h_tiles = {}
+        raw_w1 = {}
+        raw_w2 = {}
+
+        u_view = u_sb[:].rearrange("p (t k) -> p t k", t=TOKEN_TILES)
+        nc.sync.dma_start(
+            out=u_view[:, :, 0:STOCH], in_=stoch.rearrange("(p t) k -> p t k", t=TOKEN_TILES)
+        )
+        nc.sync.dma_start(
+            out=u_view[:, :, STOCH:K1], in_=action.rearrange("(p t) k -> p t k", t=TOKEN_TILES)
+        )
+        for i in range(RAW_BUFS):
+            raw_w1[i] = load_chunk(tok_w1, i)
+        nc.vector.memset(vec_rows[:], 0.0)
+        for row, vector in enumerate((tok_b1, tok_nw, tok_b2)):
+            nc.scalar.dma_start(
+                out=vec_rows[row : row + 1, :], in_=vector.rearrange("(o n) -> o n", o=1)
+            )
+
+        make_identity(nc, ident[:])
+        make_identity(nc, ident_bf[:])
+        nc.vector.memset(minus_half[:], -0.5)
+        nc.scalar.activation(out=table_warmer[:], in_=minus_half[:], func=ACT.Silu)
+
+        nc.vector.tensor_scalar(
+            out=u_view[:, :, STOCH:K1],
+            in0=u_view[:, :, STOCH:K1],
+            scalar1=1.0,
+            scalar2=-1.0,
+            op0=ALU.min,
+            op1=ALU.max,
+        )
+        for c in range(PASSES_1):
+            quantise_pass(
+                u_sb, K1, TOKEN_TILES, c, u_codes[:, c, :], u_scales[:, c, :], by_vector
+            )
+        spread_row(0, b1_all)
+        spread_row(1, nw_all)
+
+        quantise_w1_chunk(0)
+        raw_w2[0] = load_chunk(tok_w2, 0)
+        quantise_w1_chunk(1)
+        raw_w2[1] = load_chunk(tok_w2, 1)
+        layer1_products(0)
+        for i in range(CHUNKS - 1):
+            if i + 2 < CHUNKS:
+                quantise_w1_chunk(i + 2)
+                raw_w2[i + 2] = load_chunk(tok_w2, i + 2)
+            else:
+                quantise_w2_chunk(0)
+            layer1_products(i + 1)
+            layer1_statistics(i)
+        layer1_statistics(CHUNKS - 1)
+
+        nc.vector.tensor_reduce(out=row_sum[:], in_=square_sums[:], axis=AXIS.X, op=ALU.add)
+        nc.vector.tensor_scalar(
+            out=mean_eps[:],
+            in0=row_sum[:],
+            scalar1=1.0 / HIDDEN,
+            scalar2=EPS,
+            op0=ALU.mult,
+            op1=ALU.add,
+        )
+        nc.gpsimd.tensor_tensor(out=rstd[:], in0=mean_eps[:], in1=minus_half[:], op=ALU.pow)
+        spread_row(2, b2_all)
+
+        for c in range(PASSES_2):
+            quantise_chunk_pass(raw_w2[1], HIDDEN, c, w2_codes[:, 1, :, :], w2_scales[:, 1, :, :], by_both)
+            for t in range(TOKEN_TILES):
+                nc.scalar.activation(
+                    out=g_sb[:, HIDDEN * t + K_PASS * c : HIDDEN * t + K_PASS * (c + 1)],
+                    in_=gained[:, t, K_PASS * c : K_PASS * (c + 1)],
+                    func=ACT.Silu,
+                    scale=rstd[:, t : t + 1],
+                )
+            quantise_pass(
+                g_sb, HIDDEN, TOKEN_TILES, c, g_codes[:, c, :], g_scales[:, c, :], by_vector
+            )
+
+        layer2_products(0)
+        for i in range(CHUNKS - 2):
+            quantise_w2_chunk(i + 2)
+            layer2_products(i + 1)
+        layer2_products(CHUNKS - 1)

@@ -28,6 +28,9 @@ CHUNKS = HIDDEN // CHUNK
 PASSES_1 = K1 // K_PASS
 PASSES_2 = HIDDEN // K_PASS
 RAW_BUFS = 4
+ROW_PIECES = HIDDEN // CHUNK
+EARLY = 3
+PER_GROUP = 2
 
 FLOPS = 2 * TOKENS * (K1 * HIDDEN + HIDDEN * DETER)
 
@@ -49,7 +52,7 @@ def tile_mamba2backbone_pa_kernel(
 
         ident = keep.tile([P, P], F32)
         ident_bf = keep.tile([P, P], BF16)
-        vec_rows = keep.tile([P, HIDDEN], BF16)
+        vec_rows = keep.tile([P, CHUNK], BF16)
         b1_all = keep.tile([P, HIDDEN], BF16)
         nw_all = keep.tile([P, HIDDEN], BF16)
         b2_all = keep.tile([P, DETER], BF16)
@@ -71,21 +74,27 @@ def tile_mamba2backbone_pa_kernel(
         rstd = keep.tile([P, TOKEN_TILES], F32)
         table_warmer = keep.tile([P, TOKEN_TILES], F32)
 
-        def load_chunk(weight, i):
+        by_scalar = (nc.scalar.copy, nc.scalar.copy)
+        by_vector = (nc.vector.tensor_copy, nc.vector.tensor_copy)
+        h_tiles = {}
+        raw_w1 = {}
+        raw_w2 = {}
+
+        def load_chunk(weight, i, pieces):
             k = weight.shape[1]
             raw = raw_pool.tile([P, ROWS_PER_PARTITION * k], BF16, tag="raw")
-            rows = weight[CHUNK * i : CHUNK * (i + 1), :]
-            nc.sync.dma_start(
-                out=raw[:], in_=rows.rearrange("(j e) k -> j (e k)", e=ROWS_PER_PARTITION)
+            raw_rows = raw[:].rearrange("j (e k) -> j e k", e=ROWS_PER_PARTITION)
+            rows = weight[CHUNK * i : CHUNK * (i + 1), :].rearrange(
+                "(j e) k -> j e k", e=ROWS_PER_PARTITION
             )
+            for piece in range(pieces):
+                ks = slice(k // pieces * piece, k // pieces * (piece + 1))
+                nc.sync.dma_start(out=raw_rows[:, :, ks], in_=rows[:, :, ks])
             return raw
 
-        def quantise_pass(source, k, blocks, c, codes, scales, copies):
+        def transposes(source, k, blocks, c):
             words = source[:].bitcast(F32)
-            grouped = stage.tile([P, blocks * P * PACK], BF16, tag="grouped", align_bytes=64)
-            grouped_words = grouped[:].bitcast(F32).rearrange(
-                "p (b r h) -> p b r h", b=blocks, h=2
-            )
+            banks = []
             for pair in range(blocks // 2):
                 bank = psum_t.tile([P, 2, 2, P], F32, tag="bank")
                 for b in range(2):
@@ -94,37 +103,56 @@ def tile_mamba2backbone_pa_kernel(
                         nc.tensor.transpose(
                             bank[:, b, h, :], words[:, first : first + P], ident[:]
                         )
+                banks.append(bank)
+            return banks
+
+        def regroup_and_quantise(banks, codes, scales, copies):
+            blocks = 2 * len(banks)
+            grouped = stage.tile([P, blocks * P * PACK], BF16, tag="grouped", align_bytes=64)
+            grouped_words = grouped[:].bitcast(F32).rearrange(
+                "p (b r h) -> p b r h", b=blocks, h=2
+            )
+            for pair, bank in enumerate(banks):
                 copies[pair](
                     out=grouped_words[:, 2 * pair : 2 * pair + 2],
                     in_=bank[:].rearrange("p b h r -> p b r h"),
                 )
             nc.vector.quantize_mx(out=codes.bitcast(FP8X4), scales=scales, in_=grouped[:])
 
-        def quantise_chunk_pass(raw, k, c, codes, scales, copies):
-            quantise_pass(raw, k, ROWS_PER_PARTITION, c, codes[:, c, :], scales[:, c, :], copies)
+        def quantise_tokens_pass(source, k, c, codes, scales):
+            regroup_and_quantise(
+                transposes(source, k, TOKEN_TILES, c), codes[:, c, :], scales[:, c, :], by_vector
+            )
 
         def quantise_w1_chunk(i):
             for c in range(PASSES_1):
-                quantise_chunk_pass(
-                    raw_w1[i], K1, c, w1_codes[:, i, :, :], w1_scales[:, i, :, :], by_scalar
+                regroup_and_quantise(
+                    transposes(raw_w1[i], K1, ROWS_PER_PARTITION, c),
+                    w1_codes[:, i, c, :],
+                    w1_scales[:, i, c, :],
+                    by_scalar,
                 )
 
-        def quantise_w2_chunk(i):
-            for c in range(PASSES_2):
-                quantise_chunk_pass(
-                    raw_w2[i], HIDDEN, c, w2_codes[:, i, :, :], w2_scales[:, i, :, :], by_scalar
-                )
+        def w2_transposes(n):
+            return transposes(raw_w2[n // PASSES_2], HIDDEN, ROWS_PER_PARTITION, n % PASSES_2)
 
-        def spread_row(row, everywhere):
-            pick = ident_bf[:, row : row + 1].to_broadcast([P, P])
+        def w2_quantise(n, banks, copies):
+            regroup_and_quantise(
+                banks,
+                w2_codes[:, n // PASSES_2, n % PASSES_2, :],
+                w2_scales[:, n // PASSES_2, n % PASSES_2, :],
+                copies,
+            )
+
+        def spread_vector(first_row, everywhere):
             for half in range(2):
                 row_bank = psum_t.tile([P, 2 * CHUNK], BF16, tag="bank")
                 for quarter in range(2):
-                    first = 2 * CHUNK * half + CHUNK * quarter
+                    row = first_row + 2 * half + quarter
                     nc.tensor.matmul(
                         out=row_bank[:, CHUNK * quarter : CHUNK * (quarter + 1)],
-                        lhsT=pick,
-                        rhs=vec_rows[:, first : first + CHUNK],
+                        lhsT=ident_bf[:, row : row + 1].to_broadcast([P, P]),
+                        rhs=vec_rows[:],
                         start=True,
                         stop=True,
                     )
@@ -157,13 +185,14 @@ def tile_mamba2backbone_pa_kernel(
 
         def layer1_products(i):
             for t in range(TOKEN_TILES):
-                acc = products(u_codes, u_scales, w1_codes[:, i, :, :], w1_scales[:, i, :, :], PASSES_1, t)
+                acc = products(
+                    u_codes, u_scales, w1_codes[:, i, :, :], w1_scales[:, i, :, :], PASSES_1, t
+                )
                 h_biased = biased.tile([P, CHUNK], F32, tag="h_biased")
                 add_bias(h_biased[:], acc, b1_all[:, CHUNK * i : CHUNK * (i + 1)])
                 h_tiles[(i, t)] = h_biased
 
-        def layer1_statistics(i):
-            columns = slice(CHUNK * i, CHUNK * (i + 1))
+        def layer1_squares(i):
             for t in range(TOKEN_TILES):
                 squares = unread.tile([P, CHUNK], BF16, tag="squares")
                 nc.scalar.activation(
@@ -172,6 +201,10 @@ def tile_mamba2backbone_pa_kernel(
                     func=ACT.Square,
                     accum_out=square_sums[:, t, i : i + 1],
                 )
+
+        def layer1_gains(i):
+            columns = slice(CHUNK * i, CHUNK * (i + 1))
+            for t in range(TOKEN_TILES):
                 nc.vector.tensor_tensor(
                     out=gained[:, t, columns],
                     in0=h_tiles[(i, t)][:],
@@ -179,23 +212,12 @@ def tile_mamba2backbone_pa_kernel(
                     op=ALU.mult,
                 )
 
-        def layer2_products(i):
-            columns = slice(CHUNK * i, CHUNK * (i + 1))
-            out_sb = result.tile([P, TOKEN_TILES, CHUNK], F32, tag="out_sb")
-            for t in range(TOKEN_TILES):
-                acc = products(g_codes, g_scales, w2_codes[:, i, :, :], w2_scales[:, i, :, :], PASSES_2, t)
-                add_bias(out_sb[:, t, :], acc, b2_all[:, columns])
+        nc.vector.memset(vec_rows[:], 0.0)
+        for first_row, vector in ((0, tok_b1), (ROW_PIECES, tok_nw)):
             nc.sync.dma_start(
-                out=out.rearrange("(p t) n -> p t n", t=TOKEN_TILES)[:, :, columns], in_=out_sb[:]
+                out=vec_rows[first_row : first_row + ROW_PIECES, :],
+                in_=vector.rearrange("(r n) -> r n", r=ROW_PIECES),
             )
-
-        by_scalar = (nc.scalar.copy, nc.scalar.copy)
-        by_both = (nc.scalar.copy, nc.vector.tensor_copy)
-        by_vector = (nc.vector.tensor_copy,)
-        h_tiles = {}
-        raw_w1 = {}
-        raw_w2 = {}
-
         u_view = u_sb[:].rearrange("p (t k) -> p t k", t=TOKEN_TILES)
         nc.sync.dma_start(
             out=u_view[:, :, 0:STOCH], in_=stoch.rearrange("(p t) k -> p t k", t=TOKEN_TILES)
@@ -203,18 +225,17 @@ def tile_mamba2backbone_pa_kernel(
         nc.sync.dma_start(
             out=u_view[:, :, STOCH:K1], in_=action.rearrange("(p t) k -> p t k", t=TOKEN_TILES)
         )
-        for i in range(RAW_BUFS):
-            raw_w1[i] = load_chunk(tok_w1, i)
-        nc.vector.memset(vec_rows[:], 0.0)
-        for row, vector in enumerate((tok_b1, tok_nw, tok_b2)):
-            nc.scalar.dma_start(
-                out=vec_rows[row : row + 1, :], in_=vector.rearrange("(o n) -> o n", o=1)
-            )
+        raw_w1[0] = load_chunk(tok_w1, 0, PASSES_1)
+        for i in range(1, RAW_BUFS):
+            raw_w1[i] = load_chunk(tok_w1, i, 1)
 
-        make_identity(nc, ident[:])
         make_identity(nc, ident_bf[:])
+        make_identity(nc, ident[:])
         nc.vector.memset(minus_half[:], -0.5)
         nc.scalar.activation(out=table_warmer[:], in_=minus_half[:], func=ACT.Silu)
+
+        spread_vector(0, b1_all)
+        spread_vector(ROW_PIECES, nw_all)
 
         nc.vector.tensor_scalar(
             out=u_view[:, :, STOCH:K1],
@@ -225,26 +246,32 @@ def tile_mamba2backbone_pa_kernel(
             op1=ALU.max,
         )
         for c in range(PASSES_1):
-            quantise_pass(
-                u_sb, K1, TOKEN_TILES, c, u_codes[:, c, :], u_scales[:, c, :], by_vector
-            )
-        spread_row(0, b1_all)
-        spread_row(1, nw_all)
+            quantise_tokens_pass(u_sb, K1, c, u_codes, u_scales)
 
         quantise_w1_chunk(0)
-        raw_w2[0] = load_chunk(tok_w2, 0)
-        quantise_w1_chunk(1)
-        raw_w2[1] = load_chunk(tok_w2, 1)
+        raw_w2[0] = load_chunk(tok_w2, 0, 1)
         layer1_products(0)
-        for i in range(CHUNKS - 1):
-            if i + 2 < CHUNKS:
-                quantise_w1_chunk(i + 2)
-                raw_w2[i + 2] = load_chunk(tok_w2, i + 2)
-            else:
-                quantise_w2_chunk(0)
-            layer1_products(i + 1)
-            layer1_statistics(i)
-        layer1_statistics(CHUNKS - 1)
+        quantise_w1_chunk(1)
+        raw_w2[1] = load_chunk(tok_w2, 1, 1)
+        nc.sync.dma_start(out=b2_all[:], in_=tok_b2.partition_broadcast(P))
+        layer1_squares(0)
+        layer1_gains(0)
+        quantise_w1_chunk(2)
+        raw_w2[2] = load_chunk(tok_w2, 2, 1)
+        layer1_products(1)
+        quantise_w1_chunk(3)
+        raw_w2[3] = load_chunk(tok_w2, 3, 1)
+        layer1_products(2)
+        layer1_squares(1)
+        layer1_gains(1)
+        early_banks = {}
+        for n in range(EARLY):
+            early_banks[n] = w2_transposes(n)
+        layer1_products(3)
+        layer1_squares(2)
+        layer1_gains(2)
+        w2_quantise(0, early_banks[0], by_scalar)
+        layer1_squares(3)
 
         nc.vector.tensor_reduce(out=row_sum[:], in_=square_sums[:], axis=AXIS.X, op=ALU.add)
         nc.vector.tensor_scalar(
@@ -256,10 +283,12 @@ def tile_mamba2backbone_pa_kernel(
             op1=ALU.add,
         )
         nc.gpsimd.tensor_tensor(out=rstd[:], in0=mean_eps[:], in1=minus_half[:], op=ALU.pow)
-        spread_row(2, b2_all)
+        layer1_gains(3)
+        for n in range(1, EARLY):
+            w2_quantise(n, early_banks[n], by_scalar)
 
+        waiting_banks = {}
         for c in range(PASSES_2):
-            quantise_chunk_pass(raw_w2[1], HIDDEN, c, w2_codes[:, 1, :, :], w2_scales[:, 1, :, :], by_both)
             for t in range(TOKEN_TILES):
                 nc.scalar.activation(
                     out=g_sb[:, HIDDEN * t + K_PASS * c : HIDDEN * t + K_PASS * (c + 1)],
@@ -267,12 +296,26 @@ def tile_mamba2backbone_pa_kernel(
                     func=ACT.Silu,
                     scale=rstd[:, t : t + 1],
                 )
-            quantise_pass(
-                g_sb, HIDDEN, TOKEN_TILES, c, g_codes[:, c, :], g_scales[:, c, :], by_vector
-            )
+            if c < PASSES_2 // 2:
+                w2_quantise(EARLY + c, w2_transposes(EARLY + c), by_vector)
+            else:
+                waiting_banks[EARLY + c] = w2_transposes(EARLY + c)
+            quantise_tokens_pass(g_sb, HIDDEN, c, g_codes, g_scales)
+        for n in sorted(waiting_banks):
+            w2_quantise(n, waiting_banks[n], by_scalar)
 
-        layer2_products(0)
-        for i in range(CHUNKS - 2):
-            quantise_w2_chunk(i + 2)
-            layer2_products(i + 1)
-        layer2_products(CHUNKS - 1)
+        prepared = EARLY + PASSES_2
+        for i in range(CHUNKS):
+            columns = slice(CHUNK * i, CHUNK * (i + 1))
+            out_sb = result.tile([P, TOKEN_TILES, CHUNK], F32, tag="out_sb")
+            for t in range(TOKEN_TILES):
+                acc = products(
+                    g_codes, g_scales, w2_codes[:, i, :, :], w2_scales[:, i, :, :], PASSES_2, t
+                )
+                add_bias(out_sb[:, t, :], acc, b2_all[:, columns])
+                for n in range(prepared, min(prepared + PER_GROUP, CHUNKS * PASSES_2)):
+                    w2_quantise(n, w2_transposes(n), by_scalar)
+                prepared = min(prepared + PER_GROUP, CHUNKS * PASSES_2)
+            nc.sync.dma_start(
+                out=out.rearrange("(p t) n -> p t n", t=TOKEN_TILES)[:, :, columns], in_=out_sb[:]
+            )

@@ -48,7 +48,6 @@ def tile_mamba2backbone_pa_kernel(
         result = ctx.enter_context(tc.tile_pool(name="result", bufs=2))
         psum_t = ctx.enter_context(tc.psum_pool(name="psum_t", bufs=6))
         psum_acc = ctx.enter_context(tc.psum_pool(name="psum_acc", bufs=2))
-        ctx.enter_context(tc.manual_schedule())
 
         ident = keep.tile([P, P], F32)
         ident_bf = keep.tile([P, P], BF16)

@@ -29,7 +29,8 @@ PASSES_1 = K1 // K_PASS
 PASSES_2 = HIDDEN // K_PASS
 RAW_BUFS = 4
 ROW_PIECES = HIDDEN // CHUNK
-EARLY = 3
+LAG = 2
+EARLY = LAG
 PER_GROUP = 2
 
 FLOPS = 2 * TOKENS * (K1 * HIDDEN + HIDDEN * DETER)
@@ -48,6 +49,7 @@ def tile_mamba2backbone_pa_kernel(
         result = ctx.enter_context(tc.tile_pool(name="result", bufs=2))
         psum_t = ctx.enter_context(tc.psum_pool(name="psum_t", bufs=6))
         psum_acc = ctx.enter_context(tc.psum_pool(name="psum_acc", bufs=2))
+        ctx.enter_context(tc.manual_schedule())
 
         ident = keep.tile([P, P], F32)
         ident_bf = keep.tile([P, P], BF16)
@@ -76,6 +78,7 @@ def tile_mamba2backbone_pa_kernel(
         by_scalar = (nc.scalar.copy, nc.scalar.copy)
         by_vector = (nc.vector.tensor_copy, nc.vector.tensor_copy)
         h_tiles = {}
+        acc_tiles = {}
         raw_w1 = {}
         raw_w2 = {}
 
@@ -123,14 +126,16 @@ def tile_mamba2backbone_pa_kernel(
                 transposes(source, k, TOKEN_TILES, c), codes[:, c, :], scales[:, c, :], by_vector
             )
 
-        def quantise_w1_chunk(i):
-            for c in range(PASSES_1):
-                regroup_and_quantise(
-                    transposes(raw_w1[i], K1, ROWS_PER_PARTITION, c),
-                    w1_codes[:, i, c, :],
-                    w1_scales[:, i, c, :],
-                    by_scalar,
-                )
+        def w1_transposes(n):
+            return transposes(raw_w1[n // PASSES_1], K1, ROWS_PER_PARTITION, n % PASSES_1)
+
+        def w1_quantise(n, banks):
+            regroup_and_quantise(
+                banks,
+                w1_codes[:, n // PASSES_1, n % PASSES_1, :],
+                w1_scales[:, n // PASSES_1, n % PASSES_1, :],
+                by_scalar,
+            )
 
         def w2_transposes(n):
             return transposes(raw_w2[n // PASSES_2], HIDDEN, ROWS_PER_PARTITION, n % PASSES_2)
@@ -182,14 +187,27 @@ def tile_mamba2backbone_pa_kernel(
                 op=ALU.add,
             )
 
-        def layer1_products(i):
+        def layer1_products(n):
+            i = n // PASSES_1
+            c = n % PASSES_1
             for t in range(TOKEN_TILES):
-                acc = products(
-                    u_codes, u_scales, w1_codes[:, i, :, :], w1_scales[:, i, :, :], PASSES_1, t
+                if c == 0:
+                    acc = psum_acc.tile([P, CHUNK], F32, tag="acc")
+                    acc_tiles[(i, t)] = acc
+                nc.tensor.matmul_mx(
+                    out=acc_tiles[(i, t)][:],
+                    lhsT=u_codes[:, c, P * t : P * (t + 1)].bitcast(FP8X4),
+                    lhsT_scale=u_scales[:, c, P * t : P * (t + 1)],
+                    rhs=w1_codes[:, i, c, :].bitcast(FP8X4),
+                    rhs_scale=w1_scales[:, i, c, :],
+                    start=(c == 0),
+                    stop=(c == PASSES_1 - 1),
                 )
-                h_biased = biased.tile([P, CHUNK], F32, tag="h_biased")
-                add_bias(h_biased[:], acc, b1_all[:, CHUNK * i : CHUNK * (i + 1)])
-                h_tiles[(i, t)] = h_biased
+            if c == PASSES_1 - 1:
+                for t in range(TOKEN_TILES):
+                    h_biased = biased.tile([P, CHUNK], F32, tag="h_biased")
+                    add_bias(h_biased[:], acc_tiles[(i, t)], b1_all[:, CHUNK * i : CHUNK * (i + 1)])
+                    h_tiles[(i, t)] = h_biased
 
         def layer1_squares(i):
             for t in range(TOKEN_TILES):
@@ -247,30 +265,26 @@ def tile_mamba2backbone_pa_kernel(
         for c in range(PASSES_1):
             quantise_tokens_pass(u_sb, K1, c, u_codes, u_scales)
 
-        quantise_w1_chunk(0)
-        raw_w2[0] = load_chunk(tok_w2, 0, 1)
-        layer1_products(0)
-        quantise_w1_chunk(1)
-        raw_w2[1] = load_chunk(tok_w2, 1, 1)
-        nc.sync.dma_start(out=b2_all[:], in_=tok_b2.partition_broadcast(P))
-        layer1_squares(0)
-        layer1_gains(0)
-        quantise_w1_chunk(2)
-        raw_w2[2] = load_chunk(tok_w2, 2, 1)
-        layer1_products(1)
-        quantise_w1_chunk(3)
-        raw_w2[3] = load_chunk(tok_w2, 3, 1)
-        layer1_products(2)
-        layer1_squares(1)
-        layer1_gains(1)
         early_banks = {}
-        for n in range(EARLY):
-            early_banks[n] = w2_transposes(n)
-        layer1_products(3)
-        layer1_squares(2)
-        layer1_gains(2)
+        for n in range(CHUNKS * PASSES_1 + LAG):
+            if n < CHUNKS * PASSES_1:
+                banks = w1_transposes(n)
+            else:
+                early_banks[n - CHUNKS * PASSES_1] = w2_transposes(n - CHUNKS * PASSES_1)
+            if n >= LAG:
+                layer1_products(n - LAG)
+            if n < CHUNKS * PASSES_1:
+                w1_quantise(n, banks)
+                if n % PASSES_1 == PASSES_1 - 1:
+                    raw_w2[n // PASSES_1] = load_chunk(tok_w2, n // PASSES_1, 1)
+                if n == 2 * PASSES_1 - 1:
+                    nc.sync.dma_start(out=b2_all[:], in_=tok_b2.partition_broadcast(P))
+            multiplied = n - LAG - 1
+            if multiplied >= 0 and multiplied % PASSES_1 == PASSES_1 - 1:
+                layer1_squares(multiplied // PASSES_1)
+                layer1_gains(multiplied // PASSES_1)
         w2_quantise(0, early_banks[0], by_scalar)
-        layer1_squares(3)
+        layer1_squares(CHUNKS - 1)
 
         nc.vector.tensor_reduce(out=row_sum[:], in_=square_sums[:], axis=AXIS.X, op=ALU.add)
         nc.vector.tensor_scalar(
@@ -282,7 +296,7 @@ def tile_mamba2backbone_pa_kernel(
             op1=ALU.add,
         )
         nc.gpsimd.tensor_tensor(out=rstd[:], in0=mean_eps[:], in1=minus_half[:], op=ALU.pow)
-        layer1_gains(3)
+        layer1_gains(CHUNKS - 1)
         for n in range(1, EARLY):
             w2_quantise(n, early_banks[n], by_scalar)
 

@@ -43,10 +43,10 @@ def tile_mamba2backbone_pa_kernel(
     with ExitStack() as ctx:
         keep = ctx.enter_context(tc.tile_pool(name="keep", bufs=1))
         raw_pool = ctx.enter_context(tc.tile_pool(name="raw", bufs=RAW_BUFS))
-        stage = ctx.enter_context(tc.tile_pool(name="stage", bufs=4))
-        biased = ctx.enter_context(tc.tile_pool(name="biased", bufs=6))
+        stage = ctx.enter_context(tc.tile_pool(name="stage", bufs=6))
+        biased = ctx.enter_context(tc.tile_pool(name="biased", bufs=8))
         unread = ctx.enter_context(tc.tile_pool(name="unread", bufs=2))
-        result = ctx.enter_context(tc.tile_pool(name="result", bufs=2))
+        result = ctx.enter_context(tc.tile_pool(name="result", bufs=3))
         psum_t = ctx.enter_context(tc.psum_pool(name="psum_t", bufs=6))
         psum_acc = ctx.enter_context(tc.psum_pool(name="psum_acc", bufs=2))
         ctx.enter_context(tc.manual_schedule())
@@ -66,8 +66,8 @@ def tile_mamba2backbone_pa_kernel(
         w2_scales = keep.tile([P, CHUNKS, PASSES_2, CHUNK], U8, align_bytes=64)
         gained = keep.tile([P, TOKEN_TILES, HIDDEN], F32)
         g_sb = keep.tile([P, TOKEN_TILES * HIDDEN], BF16)
-        g_codes = keep.tile([P, PASSES_2, TOKENS], U32, align_bytes=64)
-        g_scales = keep.tile([P, PASSES_2, TOKENS], U8, align_bytes=64)
+        g_codes = keep.tile([P, TOKEN_TILES, PASSES_2, P], U32, align_bytes=64)
+        g_scales = keep.tile([P, TOKEN_TILES, PASSES_2, P], U8, align_bytes=64)
         square_sums = keep.tile([P, TOKEN_TILES, CHUNKS], F32)
         row_sum = keep.tile([P, TOKEN_TILES], F32)
         mean_eps = keep.tile([P, TOKEN_TILES], F32)
@@ -148,8 +148,8 @@ def tile_mamba2backbone_pa_kernel(
                 copies,
             )
 
-        def spread_vector(first_row, everywhere):
-            for half in range(2):
+        def spread_vector(first_row, everywhere, halves=(0, 1)):
+            for half in halves:
                 row_bank = psum_t.tile([P, 2 * CHUNK], BF16, tag="bank")
                 for quarter in range(2):
                     row = first_row + 2 * half + quarter
@@ -160,7 +160,7 @@ def tile_mamba2backbone_pa_kernel(
                         start=True,
                         stop=True,
                     )
-                nc.scalar.copy(
+                nc.vector.tensor_copy(
                     out=everywhere[:, 2 * CHUNK * half : 2 * CHUNK * (half + 1)], in_=row_bank[:]
                 )
 
@@ -244,91 +244,293 @@ def tile_mamba2backbone_pa_kernel(
         )
         raw_w1[0] = load_chunk(tok_w1, 0, PASSES_1)
         for i in range(1, RAW_BUFS):
-            raw_w1[i] = load_chunk(tok_w1, i, 1)
+            raw_w1[i] = load_chunk(tok_w1, i, PASSES_1)
 
         make_identity(nc, ident_bf[:])
         make_identity(nc, ident[:])
         nc.vector.memset(minus_half[:], -0.5)
         nc.scalar.activation(out=table_warmer[:], in_=minus_half[:], func=ACT.Silu)
 
-        spread_vector(0, b1_all)
-        spread_vector(ROW_PIECES, nw_all)
 
-        nc.vector.tensor_scalar(
-            out=u_view[:, :, STOCH:K1],
-            in0=u_view[:, :, STOCH:K1],
-            scalar1=1.0,
-            scalar2=-1.0,
-            op0=ALU.min,
-            op1=ALU.max,
-        )
-        for c in range(PASSES_1):
-            quantise_tokens_pass(u_sb, K1, c, u_codes, u_scales)
-
-        early_banks = {}
-        for n in range(CHUNKS * PASSES_1 + LAG):
-            if n < CHUNKS * PASSES_1:
-                banks = w1_transposes(n)
+        EN = {'S': nc.scalar.copy, 'V': nc.vector.tensor_copy}
+        banks = {}
+        grouped = {}
+        NW1 = CHUNKS * PASSES_1
+        def T(n):
+            if n < NW1:
+                banks[n] = w1_transposes(n)
             else:
-                early_banks[n - CHUNKS * PASSES_1] = w2_transposes(n - CHUNKS * PASSES_1)
-            if n >= LAG:
-                layer1_products(n - LAG)
-            if n < CHUNKS * PASSES_1:
-                w1_quantise(n, banks)
-                if n % PASSES_1 == PASSES_1 - 1:
-                    raw_w2[n // PASSES_1] = load_chunk(tok_w2, n // PASSES_1, 1)
-                if n == 2 * PASSES_1 - 1:
+                banks[n] = w2_transposes(n - NW1)
+        def C(n, e='SS'):
+            g = stage.tile([P, ROWS_PER_PARTITION * P * PACK], BF16, tag="grouped", align_bytes=64)
+            grouped[n] = g
+            for k in range(2):
+                C1(n, k, e[k])
+        def CA(n, e):
+            g = stage.tile([P, ROWS_PER_PARTITION * P * PACK], BF16, tag="grouped", align_bytes=64)
+            grouped[n] = g
+            C1(n, 0, e)
+        def CB(n, e):
+            C1(n, 1, e)
+        def C1(n, k, e):
+            gw = grouped[n][:].bitcast(F32).rearrange("p (b r h) -> p b r h", b=ROWS_PER_PARTITION, h=2)
+            EN[e](out=gw[:, 2 * k : 2 * k + 2], in_=banks[n][k][:].rearrange("p b h r -> p b r h"))
+        def Q(n):
+            if n < NW1:
+                i, c = n // PASSES_1, n % PASSES_1
+                co, sc = w1_codes[:, i, c, :], w1_scales[:, i, c, :]
+                if c == PASSES_1 - 1:
+                    raw_w2[i] = load_chunk(tok_w2, i, 1)
+                if n == 5:
                     nc.sync.dma_start(out=b2_all[:], in_=tok_b2.partition_broadcast(P))
-            multiplied = n - LAG - 1
-            if multiplied >= 0 and multiplied % PASSES_1 == PASSES_1 - 1:
-                layer1_squares(multiplied // PASSES_1)
-                layer1_gains(multiplied // PASSES_1)
-        w2_quantise(0, early_banks[0], by_scalar)
-        layer1_squares(CHUNKS - 1)
-
-        nc.vector.tensor_reduce(out=row_sum[:], in_=square_sums[:], axis=AXIS.X, op=ALU.add)
-        nc.vector.tensor_scalar(
-            out=mean_eps[:],
-            in0=row_sum[:],
-            scalar1=1.0 / HIDDEN,
-            scalar2=EPS,
-            op0=ALU.mult,
-            op1=ALU.add,
-        )
-        nc.gpsimd.tensor_tensor(out=rstd[:], in0=mean_eps[:], in1=minus_half[:], op=ALU.pow)
-        layer1_gains(CHUNKS - 1)
-        for n in range(1, EARLY):
-            w2_quantise(n, early_banks[n], by_scalar)
-
-        waiting_banks = {}
-        for c in range(PASSES_2):
-            for t in range(TOKEN_TILES):
-                nc.scalar.activation(
-                    out=g_sb[:, HIDDEN * t + K_PASS * c : HIDDEN * t + K_PASS * (c + 1)],
-                    in_=gained[:, t, K_PASS * c : K_PASS * (c + 1)],
-                    func=ACT.Silu,
-                    scale=rstd[:, t : t + 1],
-                )
-            if c < PASSES_2 // 2:
-                w2_quantise(EARLY + c, w2_transposes(EARLY + c), by_vector)
             else:
-                waiting_banks[EARLY + c] = w2_transposes(EARLY + c)
-            quantise_tokens_pass(g_sb, HIDDEN, c, g_codes, g_scales)
-        for n in sorted(waiting_banks):
-            w2_quantise(n, waiting_banks[n], by_scalar)
-
-        prepared = EARLY + PASSES_2
-        for i in range(CHUNKS):
+                i, c = (n - NW1) // PASSES_2, (n - NW1) % PASSES_2
+                co, sc = w2_codes[:, i, c, :], w2_scales[:, i, c, :]
+            nc.vector.quantize_mx(out=co.bitcast(FP8X4), scales=sc, in_=grouped[n][:])
+        def M1(i, ts, cs):
+            for t in ts:
+                if cs[0] == 0:
+                    acc = psum_acc.tile([P, CHUNK], F32, tag="acc")
+                    acc_tiles[(i, t)] = acc
+                for c in cs:
+                    nc.tensor.matmul_mx(
+                        out=acc_tiles[(i, t)][:],
+                        lhsT=u_codes[:, c, P * t : P * (t + 1)].bitcast(FP8X4),
+                        lhsT_scale=u_scales[:, c, P * t : P * (t + 1)],
+                        rhs=w1_codes[:, i, c, :].bitcast(FP8X4),
+                        rhs_scale=w1_scales[:, i, c, :],
+                        start=(c == 0), stop=(c == PASSES_1 - 1))
+        def A(i, t):
+            h_biased = biased.tile([P, CHUNK], F32, tag="h_biased")
+            add_bias(h_biased[:], acc_tiles[(i, t)], b1_all[:, CHUNK * i : CHUNK * (i + 1)])
+            h_tiles[(i, t)] = h_biased
+        def SQ(i, t):
+            squares = unread.tile([P, CHUNK], BF16, tag="squares")
+            nc.scalar.activation(out=squares[:], in_=h_tiles[(i, t)][:], func=ACT.Square,
+                accum_out=square_sums[:, t, i : i + 1])
+        def G(i, t):
             columns = slice(CHUNK * i, CHUNK * (i + 1))
-            out_sb = result.tile([P, TOKEN_TILES, CHUNK], F32, tag="out_sb")
-            for t in range(TOKEN_TILES):
-                acc = products(
-                    g_codes, g_scales, w2_codes[:, i, :, :], w2_scales[:, i, :, :], PASSES_2, t
-                )
-                add_bias(out_sb[:, t, :], acc, b2_all[:, columns])
-                for n in range(prepared, min(prepared + PER_GROUP, CHUNKS * PASSES_2)):
-                    w2_quantise(n, w2_transposes(n), by_scalar)
-                prepared = min(prepared + PER_GROUP, CHUNKS * PASSES_2)
-            nc.sync.dma_start(
-                out=out.rearrange("(p t) n -> p t n", t=TOKEN_TILES)[:, :, columns], in_=out_sb[:]
-            )
+            nc.vector.tensor_tensor(out=gained[:, t, columns], in0=h_tiles[(i, t)][:], in1=nw_all[:, columns], op=ALU.mult)
+        def N(t):
+            nc.vector.tensor_reduce(out=row_sum[:, t:t+1], in_=square_sums[:, t, :], axis=AXIS.X, op=ALU.add)
+            nc.vector.tensor_scalar(out=mean_eps[:, t:t+1], in0=row_sum[:, t:t+1], scalar1=1.0 / HIDDEN, scalar2=EPS, op0=ALU.mult, op1=ALU.add)
+            nc.gpsimd.tensor_tensor(out=rstd[:, t:t+1], in0=mean_eps[:, t:t+1], in1=minus_half[:, t:t+1], op=ALU.pow)
+        gb = {}
+        def U(t, c, w=1):
+            nc.scalar.activation(
+                out=g_sb[:, HIDDEN * t + K_PASS * c : HIDDEN * t + K_PASS * (c + w)],
+                in_=gained[:, t, K_PASS * c : K_PASS * (c + w)],
+                func=ACT.Silu, scale=rstd[:, t : t + 1])
+        def GT(t, p):
+            words = g_sb[:].bitcast(F32)
+            bank = psum_t.tile([P, 2, 2, P], F32, tag="bank")
+            for k in range(2):
+                for h in range(2):
+                    first = t * (HIDDEN // 2) + WORDS_PER_PASS * (2 * p + k) + P * h
+                    nc.tensor.transpose(bank[:, k, h, :], words[:, first : first + P], ident[:])
+            gb[(t, p)] = bank
+        def GC(t, p, e='V'):
+            g = stage.tile([P, ROWS_PER_PARTITION * P * PACK], BF16, tag="grouped", align_bytes=64)
+            grouped[('g', t, p)] = g
+            gw = g[:, 0 : 2 * P * PACK].bitcast(F32).rearrange("p (b r h) -> p b r h", b=2, h=2)
+            EN[e](out=gw, in_=gb[(t, p)][:].rearrange("p b h r -> p b r h"))
+        def GQ(t, p):
+            nc.vector.quantize_mx(
+                out=g_codes[:, t, 2 * p : 2 * p + 2, :].rearrange("p c n -> p (c n)").bitcast(FP8X4),
+                scales=g_scales[:, t, 2 * p : 2 * p + 2, :].rearrange("p c n -> p (c n)"),
+                in_=grouped[('g', t, p)][:, 0 : 2 * P * PACK])
+        acc2 = {}
+        def M2(i, t, cs=(0, 1, 2, 3)):
+            if cs[0] == 0:
+                acc = psum_acc.tile([P, CHUNK], F32, tag="acc")
+                acc2[(i, t)] = acc
+            for c in cs:
+                nc.tensor.matmul_mx(out=acc2[(i, t)][:],
+                    lhsT=g_codes[:, t, c, :].bitcast(FP8X4), lhsT_scale=g_scales[:, t, c, :],
+                    rhs=w2_codes[:, i, c, :].bitcast(FP8X4), rhs_scale=w2_scales[:, i, c, :],
+                    start=(c == 0), stop=(c == PASSES_2 - 1))
+        outv = out.rearrange("(p t) n -> p t n", t=TOKEN_TILES)
+        def O(i, t):
+            columns = slice(CHUNK * i, CHUNK * (i + 1))
+            out_sb = result.tile([P, CHUNK], F32, tag="out_sb")
+            add_bias(out_sb[:], acc2[(i, t)], b2_all[:, columns])
+            nc.sync.dma_start(out=outv[:, t, columns], in_=out_sb[:])
+
+        def UT(c):
+            ub[c] = transposes(u_sb, K1, TOKEN_TILES, c)
+        ub = {}
+        def UC(c, e):
+            g = stage.tile([P, ROWS_PER_PARTITION * P * PACK], BF16, tag="grouped", align_bytes=64)
+            grouped[('u', c)] = g
+            gw = g[:, 0 : 2 * P * PACK].bitcast(F32).rearrange("p (b r h) -> p b r h", b=2, h=2)
+            EN[e](out=gw, in_=ub[c][0][:].rearrange("p b h r -> p b r h"))
+        def UQ(c):
+            nc.vector.quantize_mx(out=u_codes[:, c, :].bitcast(FP8X4), scales=u_scales[:, c, :], in_=grouped[('u', c)][:, 0 : 2 * P * PACK])
+        def CL():
+            nc.vector.tensor_scalar(out=u_view[:, :, STOCH:K1], in0=u_view[:, :, STOCH:K1], scalar1=1.0, scalar2=-1.0, op0=ALU.min, op1=ALU.max)
+        def SP(v, h):
+            spread_vector(v * ROW_PIECES, (b1_all, nw_all)[v], (h,))
+
+        g_codes2 = g_codes[:].rearrange("p t c n -> p (t c n)").rearrange("p (c n) -> p c n", c=PASSES_2)
+        g_scales2 = g_scales[:].rearrange("p t c n -> p (t c n)").rearrange("p (c n) -> p c n", c=PASSES_2)
+        def GT2(c):
+            gb[c] = transposes(g_sb, HIDDEN, TOKEN_TILES, c)[0]
+        def GC2(c, e='V'):
+            g = stage.tile([P, ROWS_PER_PARTITION * P * PACK], BF16, tag="grouped", align_bytes=64)
+            grouped[('g', c)] = g
+            gw = g[:, 0 : 2 * P * PACK].bitcast(F32).rearrange("p (b r h) -> p b r h", b=2, h=2)
+            EN[e](out=gw, in_=gb[c][:].rearrange("p b h r -> p b r h"))
+        def GQ2(c):
+            nc.vector.quantize_mx(out=g_codes2[:, c, :].bitcast(FP8X4), scales=g_scales2[:, c, :], in_=grouped[('g', c)][:, 0 : 2 * P * PACK])
+        def M2(i, ts, cs=(0, 1, 2, 3)):
+            for t in ts:
+                if cs[0] == 0:
+                    acc = psum_acc.tile([P, CHUNK], F32, tag="acc")
+                    acc2[(i, t)] = acc
+                for c in cs:
+                    nc.tensor.matmul_mx(out=acc2[(i, t)][:],
+                        lhsT=g_codes2[:, c, P * t : P * (t + 1)].bitcast(FP8X4), lhsT_scale=g_scales2[:, c, P * t : P * (t + 1)],
+                        rhs=w2_codes[:, i, c, :].bitcast(FP8X4), rhs_scale=w2_scales[:, i, c, :],
+                        start=(c == 0), stop=(c == PASSES_2 - 1))
+
+        def TA(n):
+            words = raw_w2[(n - NW1) // PASSES_2][:].bitcast(F32)
+            bs = []
+            for pair in range(2):
+                bank = psum_acc.tile([P, 2, 2, P], F32, tag="acc")
+                for b in range(2):
+                    for h in range(2):
+                        first = (2 * pair + b) * (HIDDEN // 2) + WORDS_PER_PASS * ((n - NW1) % PASSES_2) + P * h
+                        nc.tensor.transpose(bank[:, b, h, :], words[:, first : first + P], ident[:])
+                bs.append(bank)
+            banks[n] = bs
+
+        def GT2(c):
+            words = g_sb[:].bitcast(F32)
+            bank = psum_acc.tile([P, 2, 2, P], F32, tag="acc")
+            for b in range(2):
+                for h in range(2):
+                    first = b * (HIDDEN // 2) + WORDS_PER_PASS * c + P * h
+                    nc.tensor.transpose(bank[:, b, h, :], words[:, first : first + P], ident[:])
+            gb[c] = bank
+
+
+        SP(0, 0); SP(0, 1)
+        UT(0); UC(0, 'S')
+        UT(1); UC(1, 'S')
+        SP(1, 0)
+        CL()
+        UQ(0)
+        SP(1, 1)
+        T(0)
+        UQ(1)
+        UT(2);
+        C(0, 'SV')
+        UC(2, 'S')
+        UQ(2)
+        VC = ()
+        GS = {7:(0,0),8:(0,1),10:(1,0)}
+        for n in range(1, 12):
+            T(n)
+            if n >= 4 and n % 3 == 1:
+                M1((n - 4) // 3, (0,), (0, 1, 2))
+            if n >= 5 and n % 3 == 2:
+                M1((n - 5) // 3, (1,), (0, 1, 2))
+            C(n, 'SV' if n in VC else 'SS')
+            Q(n - 1)
+            if n >= 4 and n % 3 == 1:
+                A((n - 4) // 3, 0)
+            if n >= 5 and n % 3 == 2:
+                A((n - 5) // 3, 1)
+                SQ((n - 5) // 3, 0)
+            if n >= 6 and n % 3 == 0:
+                SQ((n - 6) // 3, 1)
+            if n in GS:
+                G(*GS[n])
+
+        T(12)
+        M1(3, (0, 1), (0, 1))
+        C(12)
+        SQ(2, 1)
+        Q(11)
+        M1(3, (0, 1), (2,))
+        T(13)
+        G(1, 1)
+        A(3, 0); A(3, 1)
+        CA(13, 'S')
+        SQ(3, 0); SQ(3, 1)
+        CB(13, 'S')
+        T(14); T(15);
+        T(16)
+        G(2, 0);
+        N(0);
+        G(2, 1)
+        N(1)
+        CA(14, 'S')
+        U(0, 0); U(1, 0);
+        G(3, 0); G(3, 1)
+        U(0, 1); U(1, 1)
+        Q(12)
+        GT2(0)
+        GC2(0, 'V')
+        Q(13)
+        GQ2(0)
+        U(0, 2); U(1, 2)
+        GT2(1)
+        CB(14, 'V')
+        GC2(1, 'V')
+        Q(14)
+        GQ2(1)
+        U(0, 3); U(1, 3)
+        GT2(2)
+        C(15, 'SS')
+        GC2(2, 'V')
+        GT2(3)
+        T(17)
+        GC2(3, 'V')
+        GQ2(2)
+        M2(0, (0,1), (0,1))
+        C(16, 'SS')
+        Q(15)
+        GQ2(3)
+        T(18)
+        C(17, 'SS')
+        M2(0, (0,1), (2,3))
+        T(19)
+        Q(16)
+        C(18)
+        O(0, 0); O(0, 1)
+        T(20)
+
+        Q(17)
+        C(19)
+        Q(18)
+        M2(1, (0, 1), (0, 1))
+        Q(19)
+        T(21); T(22)
+        C(20);
+        Q(20)
+        C(21)
+        M2(1, (0, 1), (2, 3))
+        Q(21)
+        T(23); T(24)
+        C(22)
+        O(1, 0); O(1, 1)
+        Q(22)
+        M2(2, (0, 1), (0, 1))
+        C(23); Q(23)
+        T(25); T(26)
+        C(24, 'SS')
+        Q(24)
+        M2(2, (0, 1), (2, 3))
+        C(25); Q(25)
+        T(27)
+        C(26, 'SS')
+        O(2, 0);
+        Q(26)
+        O(2, 1)
+        C(27, 'SV')
+        M2(3, (0,1), (0,1,2))
+        Q(27)
+        M2(3, (0,1), (3,))
+        O(3, 0); O(3, 1)

@@ -230,7 +230,7 @@ def tile_mamba2backbone_pa_kernel(
                 )
 
         nc.vector.memset(vec_rows[:], 0.0)
-        for first_row, vector in ((0, tok_b1), (ROW_PIECES, tok_nw)):
+        for first_row, vector in ((0, tok_b1), (ROW_PIECES, tok_nw), (2 * ROW_PIECES, tok_b2)):
             nc.sync.dma_start(
                 out=vec_rows[first_row : first_row + ROW_PIECES, :],
                 in_=vector.rearrange("(r n) -> r n", r=ROW_PIECES),
@@ -244,7 +244,7 @@ def tile_mamba2backbone_pa_kernel(
         )
         raw_w1[0] = load_chunk(tok_w1, 0, PASSES_1)
         for i in range(1, RAW_BUFS):
-            raw_w1[i] = load_chunk(tok_w1, i, PASSES_1)
+            raw_w1[i] = load_chunk(tok_w1, i, PASSES_1 if i == 1 else 1)
 
         make_identity(nc, ident_bf[:])
         make_identity(nc, ident[:])
@@ -281,8 +281,6 @@ def tile_mamba2backbone_pa_kernel(
                 co, sc = w1_codes[:, i, c, :], w1_scales[:, i, c, :]
                 if c == PASSES_1 - 1:
                     raw_w2[i] = load_chunk(tok_w2, i, 1)
-                if n == 5:
-                    nc.sync.dma_start(out=b2_all[:], in_=tok_b2.partition_broadcast(P))
             else:
                 i, c = (n - NW1) // PASSES_2, (n - NW1) % PASSES_2
                 co, sc = w2_codes[:, i, c, :], w2_scales[:, i, c, :]
@@ -369,7 +367,7 @@ def tile_mamba2backbone_pa_kernel(
         def CL():
             nc.vector.tensor_scalar(out=u_view[:, :, STOCH:K1], in0=u_view[:, :, STOCH:K1], scalar1=1.0, scalar2=-1.0, op0=ALU.min, op1=ALU.max)
         def SP(v, h):
-            spread_vector(v * ROW_PIECES, (b1_all, nw_all)[v], (h,))
+            spread_vector(v * ROW_PIECES, (b1_all, nw_all, b2_all)[v], (h,))
 
         g_codes2 = g_codes[:].rearrange("p t c n -> p (t c n)").rearrange("p (c n) -> p c n", c=PASSES_2)
         g_scales2 = g_scales[:].rearrange("p t c n -> p (t c n)").rearrange("p (c n) -> p c n", c=PASSES_2)
@@ -414,6 +412,13 @@ def tile_mamba2backbone_pa_kernel(
                     nc.tensor.transpose(bank[:, b, h, :], words[:, first : first + P], ident[:])
             gb[c] = bank
 
+        def SPA(v, half):
+            row_bank = psum_acc.tile([P, 2 * CHUNK], BF16, tag="acc")
+            for quarter in range(2):
+                row = v * ROW_PIECES + 2 * half + quarter
+                nc.tensor.matmul(out=row_bank[:, CHUNK * quarter : CHUNK * (quarter + 1)], lhsT=ident_bf[:, row : row + 1].to_broadcast([P, P]), rhs=vec_rows[:], start=True, stop=True)
+            EN['S'](out=b2_all[:, 2 * CHUNK * half : 2 * CHUNK * (half + 1)], in_=row_bank[:])
+
 
         SP(0, 0); SP(0, 1)
         UT(0); UC(0, 'S')
@@ -428,6 +433,7 @@ def tile_mamba2backbone_pa_kernel(
         C(0, 'SV')
         UC(2, 'S')
         UQ(2)
+        SP(2, 0); SP(2, 1)
         VC = ()
         GS = {7:(0,0),8:(0,1),10:(1,0)}
         for n in range(1, 12):

@@ -44,7 +44,7 @@ def tile_mamba2backbone_pa_kernel(
         keep = ctx.enter_context(tc.tile_pool(name="keep", bufs=1))
         raw_pool = ctx.enter_context(tc.tile_pool(name="raw", bufs=RAW_BUFS))
         stage = ctx.enter_context(tc.tile_pool(name="stage", bufs=6))
-        biased = ctx.enter_context(tc.tile_pool(name="biased", bufs=8))
+        biased = ctx.enter_context(tc.tile_pool(name="biased", bufs=6))
         unread = ctx.enter_context(tc.tile_pool(name="unread", bufs=2))
         result = ctx.enter_context(tc.tile_pool(name="result", bufs=3))
         psum_t = ctx.enter_context(tc.psum_pool(name="psum_t", bufs=6))
@@ -419,6 +419,18 @@ def tile_mamba2backbone_pa_kernel(
                 nc.tensor.matmul(out=row_bank[:, CHUNK * quarter : CHUNK * (quarter + 1)], lhsT=ident_bf[:, row : row + 1].to_broadcast([P, P]), rhs=vec_rows[:], start=True, stop=True)
             EN['S'](out=b2_all[:, 2 * CHUNK * half : 2 * CHUNK * (half + 1)], in_=row_bank[:])
 
+        def MP(n):
+            i, c = n // PASSES_1, n % PASSES_1
+            M1(i, (0, 1), (c,))
+
+        def MP2(m):
+            M2(m // PASSES_2, (0, 1), (m % PASSES_2,))
+
+        def NB():
+            nc.vector.tensor_reduce(out=row_sum[:], in_=square_sums[:], axis=AXIS.X, op=ALU.add)
+            nc.vector.tensor_scalar(out=mean_eps[:], in0=row_sum[:], scalar1=1.0 / HIDDEN, scalar2=EPS, op0=ALU.mult, op1=ALU.add)
+            nc.gpsimd.tensor_tensor(out=rstd[:], in0=mean_eps[:], in1=minus_half[:], op=ALU.pow)
+
 
         SP(0, 0); SP(0, 1)
         UT(0); UC(0, 'S')
@@ -468,11 +480,12 @@ def tile_mamba2backbone_pa_kernel(
         CB(13, 'S')
         T(14); T(15);
         T(16)
-        G(2, 0);
-        N(0);
+        G(2, 0)
         G(2, 1)
-        N(1)
-        CA(14, 'S')
+        NB()
+        C(14, 'VV')
+        T(17)
+        CA(15, 'S')
         U(0, 0); U(1, 0);
         G(3, 0); G(3, 1)
         U(0, 1); U(1, 1)
@@ -483,22 +496,20 @@ def tile_mamba2backbone_pa_kernel(
         GQ2(0)
         U(0, 2); U(1, 2)
         GT2(1)
-        CB(14, 'V')
         GC2(1, 'V')
         Q(14)
         GQ2(1)
         U(0, 3); U(1, 3)
         GT2(2)
-        C(15, 'SS')
-        GC2(2, 'V')
+        GC2(2, 'S')
         GT2(3)
-        T(17)
-        GC2(3, 'V')
+        GC2(3, 'S')
         GQ2(2)
         M2(0, (0,1), (0,1))
-        C(16, 'SS')
-        Q(15)
+        CB(15, 'S')
         GQ2(3)
+        Q(15)
+        C(16, 'SS')
         T(18)
         C(17, 'SS')
         M2(0, (0,1), (2,3))

@@ -431,6 +431,28 @@ def tile_mamba2backbone_pa_kernel(
             nc.vector.tensor_scalar(out=mean_eps[:], in0=row_sum[:], scalar1=1.0 / HIDDEN, scalar2=EPS, op0=ALU.mult, op1=ALU.add)
             nc.gpsimd.tensor_tensor(out=rstd[:], in0=mean_eps[:], in1=minus_half[:], op=ALU.pow)
 
+        def SA(v, half):
+            row_bank = psum_acc.tile([P, 2 * CHUNK], BF16, tag="acc")
+            for quarter in range(2):
+                row = v * ROW_PIECES + 2 * half + quarter
+                nc.tensor.matmul(out=row_bank[:, CHUNK * quarter : CHUNK * (quarter + 1)], lhsT=ident_bf[:, row : row + 1].to_broadcast([P, P]), rhs=vec_rows[:], start=True, stop=True)
+            nc.vector.tensor_copy(out=(b1_all, nw_all, b2_all)[v][:, 2 * CHUNK * half : 2 * CHUNK * (half + 1)], in_=row_bank[:])
+
+        def DM(c, k):
+            bank = psum_acc.tile([P, 2, 2, P], F32, tag="acc")
+            gb[c] = bank
+            for _ in range(k):
+                nc.tensor.matmul(out=bank[:].rearrange("p b h r -> p (b h r)"), lhsT=ident_bf[:], rhs=vec_rows[:], start=True, stop=True)
+        def GT2(c):
+            words = g_sb[:].bitcast(F32)
+            if c not in gb:
+                bank = psum_acc.tile([P, 2, 2, P], F32, tag="acc")
+                gb[c] = bank
+            for b in range(2):
+                for h in range(2):
+                    first = b * (HIDDEN // 2) + WORDS_PER_PASS * c + P * h
+                    nc.tensor.transpose(gb[c][:, b, h, :], words[:, first : first + P], ident[:])
+
 
         SP(0, 0); SP(0, 1)
         UT(0); UC(0, 'S')
@@ -490,16 +512,19 @@ def tile_mamba2backbone_pa_kernel(
         G(3, 0); G(3, 1)
         U(0, 1); U(1, 1)
         Q(12)
+        DM(0, 2)
         GT2(0)
         GC2(0, 'V')
         Q(13)
         GQ2(0)
         U(0, 2); U(1, 2)
+        DM(1, 2)
         GT2(1)
         GC2(1, 'V')
         Q(14)
         GQ2(1)
         U(0, 3); U(1, 3)
+        DM(2, 2)
         GT2(2)
         GC2(2, 'S')
         GT2(3)

@@ -46,7 +46,7 @@ def tile_mamba2backbone_pa_kernel(
         stage = ctx.enter_context(tc.tile_pool(name="stage", bufs=6))
         biased = ctx.enter_context(tc.tile_pool(name="biased", bufs=6))
         unread = ctx.enter_context(tc.tile_pool(name="unread", bufs=2))
-        result = ctx.enter_context(tc.tile_pool(name="result", bufs=3))
+        result = ctx.enter_context(tc.tile_pool(name="result", bufs=5))
         psum_t = ctx.enter_context(tc.psum_pool(name="psum_t", bufs=6))
         psum_acc = ctx.enter_context(tc.psum_pool(name="psum_acc", bufs=2))
         ctx.enter_context(tc.manual_schedule())
@@ -230,7 +230,7 @@ def tile_mamba2backbone_pa_kernel(
                 )
 
         nc.vector.memset(vec_rows[:], 0.0)
-        for first_row, vector in ((0, tok_b1), (ROW_PIECES, tok_nw), (2 * ROW_PIECES, tok_b2)):
+        for first_row, vector in ((0, tok_b1), (ROW_PIECES, tok_nw)):
             nc.sync.dma_start(
                 out=vec_rows[first_row : first_row + ROW_PIECES, :],
                 in_=vector.rearrange("(r n) -> r n", r=ROW_PIECES),
@@ -242,9 +242,14 @@ def tile_mamba2backbone_pa_kernel(
         nc.sync.dma_start(
             out=u_view[:, :, STOCH:K1], in_=action.rearrange("(p t) k -> p t k", t=TOKEN_TILES)
         )
-        raw_w1[0] = load_chunk(tok_w1, 0, PASSES_1)
-        for i in range(1, RAW_BUFS):
-            raw_w1[i] = load_chunk(tok_w1, i, PASSES_1 if i == 1 else 1)
+        PARTS = (((0, 2), (2, 3)), ((0, 2), (2, 3)), ((0, 3),), ((0, 3),))
+        for i in range(RAW_BUFS):
+            rawi = raw_pool.tile([P, ROWS_PER_PARTITION * K1], BF16, tag="raw")
+            raw_w1[i] = rawi
+            for c0, c1 in PARTS[i]:
+                nc.sync.dma_start(
+                    out=rawi[:].rearrange("j (e k) -> j e k", e=ROWS_PER_PARTITION)[:, :, K_PASS * c0 : K_PASS * c1],
+                    in_=tok_w1[CHUNK * i : CHUNK * (i + 1), :].rearrange("(j e) k -> j e k", e=ROWS_PER_PARTITION)[:, :, K_PASS * c0 : K_PASS * c1])
 
         make_identity(nc, ident_bf[:])
         make_identity(nc, ident[:])
@@ -281,6 +286,8 @@ def tile_mamba2backbone_pa_kernel(
                 co, sc = w1_codes[:, i, c, :], w1_scales[:, i, c, :]
                 if c == PASSES_1 - 1:
                     raw_w2[i] = load_chunk(tok_w2, i, 1)
+                    if i == 2:
+                        nc.sync.dma_start(out=b2_all[:], in_=tok_b2.partition_broadcast(P))
             else:
                 i, c = (n - NW1) // PASSES_2, (n - NW1) % PASSES_2
                 co, sc = w2_codes[:, i, c, :], w2_scales[:, i, c, :]
@@ -453,6 +460,42 @@ def tile_mamba2backbone_pa_kernel(
                     first = b * (HIDDEN // 2) + WORDS_PER_PASS * c + P * h
                     nc.tensor.transpose(gb[c][:, b, h, :], words[:, first : first + P], ident[:])
 
+        def TB(n, k):
+            words = raw_w2[(n - NW1) // PASSES_2][:].bitcast(F32)
+            bank = psum_t.tile([P, 2, 2, P], F32, tag="bank")
+            for b in range(2):
+                for h in range(2):
+                    first = (2 * k + b) * (HIDDEN // 2) + WORDS_PER_PASS * ((n - NW1) % PASSES_2) + P * h
+                    nc.tensor.transpose(bank[:, b, h, :], words[:, first : first + P], ident[:])
+            banks.setdefault(n, []).append(bank)
+        def X(a, b):
+            for k in range(a, b):
+                i, c, t = k // 8, k % 8 // 2, k % 2
+                M2(i, (t,), (c,))
+
+        def ML(ts, cs):
+            for c in cs:
+                for t in ts:
+                    if c == 0:
+                        acc = psum_t.tile([P, CHUNK], F32, tag="bank")
+                        acc2[(3, t)] = acc
+                    nc.tensor.matmul_mx(out=acc2[(3, t)][:],
+                        lhsT=g_codes2[:, c, P * t : P * (t + 1)].bitcast(FP8X4), lhsT_scale=g_scales2[:, c, P * t : P * (t + 1)],
+                        rhs=w2_codes[:, 3, c, :].bitcast(FP8X4), rhs_scale=w2_scales[:, 3, c, :],
+                        start=(c == 0), stop=(c == PASSES_2 - 1))
+
+        def DX(c, k):
+            if c not in gb:
+                bank = psum_acc.tile([P, 2, 2, P], F32, tag="acc")
+                gb[c] = bank
+            for _ in range(k):
+                nc.tensor.matmul(out=gb[c][:].rearrange("p b h r -> p (b h r)"), lhsT=ident_bf[:], rhs=vec_rows[:], start=True, stop=True)
+
+        def D1(k):
+            idle = psum_acc.tile([P, CHUNK], F32, tag="acc")
+            for _ in range(k):
+                nc.tensor.matmul(out=idle[:], lhsT=ident_bf[:], rhs=vec_rows[:], start=True, stop=True)
+
 
         SP(0, 0); SP(0, 1)
         UT(0); UC(0, 'S')
@@ -467,7 +510,6 @@ def tile_mamba2backbone_pa_kernel(
         C(0, 'SV')
         UC(2, 'S')
         UQ(2)
-        SP(2, 0); SP(2, 1)
         VC = ()
         GS = {7:(0,0),8:(0,1),10:(1,0)}
         for n in range(1, 12):
@@ -500,57 +542,58 @@ def tile_mamba2backbone_pa_kernel(
         CA(13, 'S')
         SQ(3, 0); SQ(3, 1)
         CB(13, 'S')
-        T(14); T(15);
+        T(14); T(15)
+        DX(0, 2)
         T(16)
         G(2, 0)
         G(2, 1)
         NB()
         C(14, 'VV')
         T(17)
-        CA(15, 'S')
-        U(0, 0); U(1, 0);
+        C(15, 'SS')
+        CA(16, 'S')
+        T(18)
+        U(0, 0); U(1, 0)
         G(3, 0); G(3, 1)
         U(0, 1); U(1, 1)
         Q(12)
-        DM(0, 2)
+        Q(13)
+        DX(0, 1)
         GT2(0)
         GC2(0, 'V')
-        Q(13)
+        Q(14)
         GQ2(0)
         U(0, 2); U(1, 2)
-        DM(1, 2)
+        DX(1, 2)
         GT2(1)
         GC2(1, 'V')
-        Q(14)
+        Q(15)
         GQ2(1)
         U(0, 3); U(1, 3)
-        DM(2, 2)
+        DX(2, 1)
         GT2(2)
         GC2(2, 'S')
+        DX(3, 1)
         GT2(3)
         GC2(3, 'S')
         GQ2(2)
-        M2(0, (0,1), (0,1))
-        CB(15, 'S')
         GQ2(3)
-        Q(15)
-        C(16, 'SS')
-        T(18)
+        M2(0, (0,1), (0,1))
+        CB(16, 'S')
         C(17, 'SS')
+        Q(16)
         M2(0, (0,1), (2,3))
         T(19)
-        Q(16)
         C(18)
         O(0, 0); O(0, 1)
         T(20)
-
         Q(17)
         C(19)
         Q(18)
         M2(1, (0, 1), (0, 1))
         Q(19)
         T(21); T(22)
-        C(20);
+        C(20)
         Q(20)
         C(21)
         M2(1, (0, 1), (2, 3))
@@ -568,11 +611,11 @@ def tile_mamba2backbone_pa_kernel(
         C(25); Q(25)
         T(27)
         C(26, 'SS')
-        O(2, 0);
         Q(26)
-        O(2, 1)
-        C(27, 'SV')
-        M2(3, (0,1), (0,1,2))
+        C(27, 'SS')
+        O(2, 0)
+        ML((0, 1), (0, 1, 2))
         Q(27)
-        M2(3, (0,1), (3,))
+        O(2, 1)
+        ML((0, 1), (3,))
         O(3, 0); O(3, 1)

@@ -242,7 +242,7 @@ def tile_mamba2backbone_pa_kernel(
         nc.sync.dma_start(
             out=u_view[:, :, STOCH:K1], in_=action.rearrange("(p t) k -> p t k", t=TOKEN_TILES)
         )
-        PARTS = (((0, 2), (2, 3)), ((0, 2), (2, 3)), ((0, 3),), ((0, 3),))
+        PARTS = (((0, 1), (1, 3)), ((0, 2), (2, 3)), ((0, 3),), ((0, 3),))
         for i in range(RAW_BUFS):
             rawi = raw_pool.tile([P, ROWS_PER_PARTITION * K1], BF16, tag="raw")
             raw_w1[i] = rawi
@@ -510,9 +510,11 @@ def tile_mamba2backbone_pa_kernel(
         C(0, 'SV')
         UC(2, 'S')
         UQ(2)
-        VC = ()
-        GS = {7:(0,0),8:(0,1),10:(1,0)}
+        VC = (8,)
+        GS = {6:(0,0),9:(0,1)}
         for n in range(1, 12):
+            if n == 3:
+                D1(2)
             T(n)
             if n >= 4 and n % 3 == 1:
                 M1((n - 4) // 3, (0,), (0, 1, 2))
@@ -523,10 +525,17 @@ def tile_mamba2backbone_pa_kernel(
             if n >= 4 and n % 3 == 1:
                 A((n - 4) // 3, 0)
             if n >= 5 and n % 3 == 2:
-                A((n - 5) // 3, 1)
-                SQ((n - 5) // 3, 0)
-            if n >= 6 and n % 3 == 0:
-                SQ((n - 6) // 3, 1)
+                if (n - 5) // 3 not in (0, 1):
+                    A((n - 5) // 3, 1)
+                if n < 11:
+                    SQ((n - 5) // 3, 0)
+            if n in (6, 9) and (n - 6) // 3 in (0, 1):
+                A((n - 6) // 3, 1)
+            if n == 6:
+                SQ(0, 1)
+            if n == 11:
+                SQ(1, 1)
+                SQ(2, 0)
             if n in GS:
                 G(*GS[n])
 
@@ -537,6 +546,7 @@ def tile_mamba2backbone_pa_kernel(
         Q(11)
         M1(3, (0, 1), (2,))
         T(13)
+        G(1, 0)
         G(1, 1)
         A(3, 0); A(3, 1)
         CA(13, 'S')
@@ -570,7 +580,7 @@ def tile_mamba2backbone_pa_kernel(
         Q(15)
         GQ2(1)
         U(0, 3); U(1, 3)
-        DX(2, 1)
+        DX(2, 2)
         GT2(2)
         GC2(2, 'S')
         DX(3, 1)
@@ -585,9 +595,10 @@ def tile_mamba2backbone_pa_kernel(
         M2(0, (0,1), (2,3))
         T(19)
         C(18)
-        O(0, 0); O(0, 1)
-        T(20)
+        O(0, 0)
         Q(17)
+        O(0, 1)
+        T(20)
         C(19)
         Q(18)
         M2(1, (0, 1), (0, 1))
@@ -611,11 +622,11 @@ def tile_mamba2backbone_pa_kernel(
         C(25); Q(25)
         T(27)
         C(26, 'SS')
+        O(2, 0)
         Q(26)
         C(27, 'SS')
-        O(2, 0)
+        O(2, 1)
         ML((0, 1), (0, 1, 2))
         Q(27)
-        O(2, 1)
         ML((0, 1), (3,))
         O(3, 0); O(3, 1)

@@ -242,14 +242,13 @@ def tile_mamba2backbone_pa_kernel(
         nc.sync.dma_start(
             out=u_view[:, :, STOCH:K1], in_=action.rearrange("(p t) k -> p t k", t=TOKEN_TILES)
         )
-        PARTS = (((0, 1), (1, 3)), ((0, 2), (2, 3)), ((0, 3),), ((0, 3),))
         for i in range(RAW_BUFS):
             rawi = raw_pool.tile([P, ROWS_PER_PARTITION * K1], BF16, tag="raw")
             raw_w1[i] = rawi
-            for c0, c1 in PARTS[i]:
+            for k in range(2):
                 nc.sync.dma_start(
-                    out=rawi[:].rearrange("j (e k) -> j e k", e=ROWS_PER_PARTITION)[:, :, K_PASS * c0 : K_PASS * c1],
-                    in_=tok_w1[CHUNK * i : CHUNK * (i + 1), :].rearrange("(j e) k -> j e k", e=ROWS_PER_PARTITION)[:, :, K_PASS * c0 : K_PASS * c1])
+                    out=rawi[:].rearrange("j (e k) -> j e k", e=ROWS_PER_PARTITION)[:, 2 * k : 2 * k + 2, :],
+                    in_=tok_w1[CHUNK * i : CHUNK * (i + 1), :].rearrange("(j e) k -> j e k", e=ROWS_PER_PARTITION)[:, 2 * k : 2 * k + 2, :])
 
         make_identity(nc, ident_bf[:])
         make_identity(nc, ident[:])
@@ -496,57 +495,104 @@ def tile_mamba2backbone_pa_kernel(
             for _ in range(k):
                 nc.tensor.matmul(out=idle[:], lhsT=ident_bf[:], rhs=vec_rows[:], start=True, stop=True)
 
+        def NA(t):
+            nc.vector.tensor_scalar(out=scaled[:, t, :], in0=square_sums[:, t, :], scalar1=1.0 / HIDDEN, scalar2=EPS, op0=ALU.mult, op1=ALU.add, accum_out=mean_eps[:, t : t + 1])
+        def NP():
+            nc.gpsimd.tensor_tensor(out=rstd[:], in0=mean_eps[:], in1=minus_half[:], op=ALU.pow)
+        scaled = keep.tile([P, TOKEN_TILES, CHUNKS], F32)
 
-        SP(0, 0); SP(0, 1)
+        def H(m):
+            i, k, c = m // 6, m % 6 // 3, m % 3
+            n = 3 * i + c
+            words = raw_w1[i][:].bitcast(F32)
+            bank = psum_t.tile([P, 2, 2, P], F32, tag="bank")
+            for b in range(2):
+                for h in range(2):
+                    first = (2 * k + b) * (K1 // 2) + WORDS_PER_PASS * c + P * h
+                    nc.tensor.transpose(bank[:, b, h, :], words[:, first : first + P], ident[:])
+            banks.setdefault(n, []).append(bank)
+        def HC(m, e='S'):
+            i, k, c = m // 6, m % 6 // 3, m % 3
+            n = 3 * i + c
+            if k == 0:
+                g = stage.tile([P, ROWS_PER_PARTITION * P * PACK], BF16, tag="grouped", align_bytes=64)
+                grouped[n] = g
+            C1(n, k, e)
+        def H3(i, k):
+            for c in range(3):
+                H(6 * i + 3 * k + c)
+        def C3(i, k, e='SSS'):
+            for c in range(3):
+                HC(6 * i + 3 * k + c, e[c])
+
+
+        SA(0, 0); SA(0, 1)
         UT(0); UC(0, 'S')
         UT(1); UC(1, 'S')
-        SP(1, 0)
-        CL()
+        SA(1, 0)
+        H3(0, 0)
         UQ(0)
-        SP(1, 1)
-        T(0)
+        CL()
         UQ(1)
-        UT(2);
-        C(0, 'SV')
+        SA(1, 1)
+        C3(0, 0)
+        H3(0, 1)
+        C3(0, 1)
+        UT(2)
+        Q(0)
         UC(2, 'S')
+        D1(1)
+        H3(1, 0)
+        D1(2)
+        Q(1)
         UQ(2)
-        VC = (8,)
-        GS = {6:(0,0),9:(0,1)}
-        for n in range(1, 12):
-            if n == 3:
-                D1(2)
-            T(n)
-            if n >= 4 and n % 3 == 1:
-                M1((n - 4) // 3, (0,), (0, 1, 2))
-            if n >= 5 and n % 3 == 2:
-                M1((n - 5) // 3, (1,), (0, 1, 2))
-            C(n, 'SV' if n in VC else 'SS')
-            Q(n - 1)
-            if n >= 4 and n % 3 == 1:
-                A((n - 4) // 3, 0)
-            if n >= 5 and n % 3 == 2:
-                if (n - 5) // 3 not in (0, 1):
-                    A((n - 5) // 3, 1)
-                if n < 11:
-                    SQ((n - 5) // 3, 0)
-            if n in (6, 9) and (n - 6) // 3 in (0, 1):
-                A((n - 6) // 3, 1)
-            if n == 6:
-                SQ(0, 1)
-            if n == 11:
-                SQ(1, 1)
-                SQ(2, 0)
-            if n in GS:
-                G(*GS[n])
-
+        Q(2)
+        C3(1, 0, 'SSV')
+        H3(1, 1)
+        M1(0, (0,), (0, 1, 2))
+        C3(1, 1)
+        Q(3)
+        A(0, 0)
+        Q(4)
+        H3(2, 0)
+        M1(0, (1,), (0, 1, 2))
+        Q(5)
+        A(0, 1)
+        C3(2, 0)
+        SQ(0, 0)
+        G(0, 0)
+        H3(2, 1)
+        M1(1, (0,), (0, 1, 2))
+        G(0, 1)
+        C3(2, 1)
+        SQ(0, 1)
+        A(1, 0)
+        Q(6); Q(7)
+        H3(3, 0)
+        M1(1, (1,), (0, 1, 2))
+        C3(3, 0)
+        Q(8)
+        A(1, 1)
+        H3(3, 1)
+        M1(2, (0,), (0, 1, 2))
+        G(1, 0)
+        C3(3, 1)
+        A(2, 0)
+        Q(9)
+        SQ(1, 0)
+        SQ(1, 1)
+        M1(2, (1,), (0, 1, 2))
         T(12)
+        Q(10)
+        SQ(2, 0)
+        A(2, 1)
+
         M1(3, (0, 1), (0, 1))
         C(12)
         SQ(2, 1)
         Q(11)
         M1(3, (0, 1), (2,))
         T(13)
-        G(1, 0)
         G(1, 1)
         A(3, 0); A(3, 1)
         CA(13, 'S')
@@ -588,11 +634,12 @@ def tile_mamba2backbone_pa_kernel(
         GC2(3, 'S')
         GQ2(2)
         GQ2(3)
-        M2(0, (0,1), (0,1))
+        M2(0, (0,), (0, 1, 2))
         CB(16, 'S')
         C(17, 'SS')
         Q(16)
-        M2(0, (0,1), (2,3))
+        M2(0, (1,), (0, 1, 2))
+        M2(0, (0, 1), (3,))
         T(19)
         C(18)
         O(0, 0)

from contextlib import ExitStack

import concourse.mybir as mybir
from concourse.masks import make_identity

F32 = mybir.dt.float32
BF16 = mybir.dt.bfloat16
U32 = mybir.dt.uint32
U8 = mybir.dt.uint8
FP8X4 = mybir.dt.float8_e4m3fn_x4
ALU = mybir.AluOpType
ACT = mybir.ActivationFunctionType
AXIS = mybir.AxisListType

P = 128
PACK = 4
K_PASS = P * PACK
WORDS_PER_PASS = K_PASS // 2

TOKENS, STOCH, ACT_DIM, HIDDEN, DETER = 256, 1024, 512, 2048, 2048
K1 = STOCH + ACT_DIM
EPS = 1e-4
TOKEN_TILES = TOKENS // P

CHUNK = 512
ROWS_PER_PARTITION = CHUNK // P
CHUNKS = HIDDEN // CHUNK
PASSES_1 = K1 // K_PASS
PASSES_2 = HIDDEN // K_PASS
RAW_BUFS = 4
ROW_PIECES = HIDDEN // CHUNK
LAG = 2
EARLY = LAG
PER_GROUP = 2

FLOPS = 2 * TOKENS * (K1 * HIDDEN + HIDDEN * DETER)


def tile_mamba2backbone_pa_kernel(
    tc, stoch, action, tok_w1, tok_b1, tok_nw, tok_w2, tok_b2, out
):
    nc = tc.nc
    with ExitStack() as ctx:
        keep = ctx.enter_context(tc.tile_pool(name="keep", bufs=1))
        raw_pool = ctx.enter_context(tc.tile_pool(name="raw", bufs=RAW_BUFS))
        stage = ctx.enter_context(tc.tile_pool(name="stage", bufs=6))
        biased = ctx.enter_context(tc.tile_pool(name="biased", bufs=6))
        unread = ctx.enter_context(tc.tile_pool(name="unread", bufs=2))
        result = ctx.enter_context(tc.tile_pool(name="result", bufs=5))
        psum_t = ctx.enter_context(tc.psum_pool(name="psum_t", bufs=6))
        psum_acc = ctx.enter_context(tc.psum_pool(name="psum_acc", bufs=2))
        ctx.enter_context(tc.manual_schedule())

        ident = keep.tile([P, P], F32)
        ident_bf = keep.tile([P, P], BF16)
        vec_rows = keep.tile([P, CHUNK], BF16)
        b1_all = keep.tile([P, HIDDEN], BF16)
        nw_all = keep.tile([P, HIDDEN], BF16)
        b2_all = keep.tile([P, DETER], BF16)
        u_sb = keep.tile([P, TOKEN_TILES * K1], BF16)
        u_codes = keep.tile([P, PASSES_1, TOKENS], U32, align_bytes=64)
        u_scales = keep.tile([P, PASSES_1, TOKENS], U8, align_bytes=64)
        w1_codes = keep.tile([P, CHUNKS, PASSES_1, CHUNK], U32, align_bytes=64)
        w1_scales = keep.tile([P, CHUNKS, PASSES_1, CHUNK], U8, align_bytes=64)
        w2_codes = keep.tile([P, CHUNKS, PASSES_2, CHUNK], U32, align_bytes=64)
        w2_scales = keep.tile([P, CHUNKS, PASSES_2, CHUNK], U8, align_bytes=64)
        gained = keep.tile([P, TOKEN_TILES, HIDDEN], F32)
        g_sb = keep.tile([P, TOKEN_TILES * HIDDEN], BF16)
        g_codes = keep.tile([P, TOKEN_TILES, PASSES_2, P], U32, align_bytes=64)
        g_scales = keep.tile([P, TOKEN_TILES, PASSES_2, P], U8, align_bytes=64)
        square_sums = keep.tile([P, TOKEN_TILES, CHUNKS], F32)
        row_sum = keep.tile([P, TOKEN_TILES], F32)
        mean_eps = keep.tile([P, TOKEN_TILES], F32)
        minus_half = keep.tile([P, TOKEN_TILES], F32)
        rstd = keep.tile([P, TOKEN_TILES], F32)
        table_warmer = keep.tile([P, TOKEN_TILES], F32)

        by_scalar = (nc.scalar.copy, nc.scalar.copy)
        by_vector = (nc.vector.tensor_copy, nc.vector.tensor_copy)
        h_tiles = {}
        acc_tiles = {}
        raw_w1 = {}
        raw_w2 = {}

        def load_chunk(weight, i, pieces):
            k = weight.shape[1]
            raw = raw_pool.tile([P, ROWS_PER_PARTITION * k], BF16, tag="raw")
            raw_rows = raw[:].rearrange("j (e k) -> j e k", e=ROWS_PER_PARTITION)
            rows = weight[CHUNK * i : CHUNK * (i + 1), :].rearrange(
                "(j e) k -> j e k", e=ROWS_PER_PARTITION
            )
            for piece in range(pieces):
                ks = slice(k // pieces * piece, k // pieces * (piece + 1))
                nc.sync.dma_start(out=raw_rows[:, :, ks], in_=rows[:, :, ks])
            return raw

        def transposes(source, k, blocks, c):
            words = source[:].bitcast(F32)
            banks = []
            for pair in range(blocks // 2):
                bank = psum_t.tile([P, 2, 2, P], F32, tag="bank")
                for b in range(2):
                    for h in range(2):
                        first = (2 * pair + b) * (k // 2) + WORDS_PER_PASS * c + P * h
                        nc.tensor.transpose(
                            bank[:, b, h, :], words[:, first : first + P], ident[:]
                        )
                banks.append(bank)
            return banks

        def regroup_and_quantise(banks, codes, scales, copies):
            blocks = 2 * len(banks)
            grouped = stage.tile([P, blocks * P * PACK], BF16, tag="grouped", align_bytes=64)
            grouped_words = grouped[:].bitcast(F32).rearrange(
                "p (b r h) -> p b r h", b=blocks, h=2
            )
            for pair, bank in enumerate(banks):
                copies[pair](
                    out=grouped_words[:, 2 * pair : 2 * pair + 2],
                    in_=bank[:].rearrange("p b h r -> p b r h"),
                )
            nc.vector.quantize_mx(out=codes.bitcast(FP8X4), scales=scales, in_=grouped[:])

        def quantise_tokens_pass(source, k, c, codes, scales):
            regroup_and_quantise(
                transposes(source, k, TOKEN_TILES, c), codes[:, c, :], scales[:, c, :], by_vector
            )

        def w1_transposes(n):
            return transposes(raw_w1[n // PASSES_1], K1, ROWS_PER_PARTITION, n % PASSES_1)

        def w1_quantise(n, banks):
            regroup_and_quantise(
                banks,
                w1_codes[:, n // PASSES_1, n % PASSES_1, :],
                w1_scales[:, n // PASSES_1, n % PASSES_1, :],
                by_scalar,
            )

        def w2_transposes(n):
            return transposes(raw_w2[n // PASSES_2], HIDDEN, ROWS_PER_PARTITION, n % PASSES_2)

        def w2_quantise(n, banks, copies):
            regroup_and_quantise(
                banks,
                w2_codes[:, n // PASSES_2, n % PASSES_2, :],
                w2_scales[:, n // PASSES_2, n % PASSES_2, :],
                copies,
            )

        def spread_vector(first_row, everywhere, halves=(0, 1)):
            for half in halves:
                row_bank = psum_t.tile([P, 2 * CHUNK], BF16, tag="bank")
                for quarter in range(2):
                    row = first_row + 2 * half + quarter
                    nc.tensor.matmul(
                        out=row_bank[:, CHUNK * quarter : CHUNK * (quarter + 1)],
                        lhsT=ident_bf[:, row : row + 1].to_broadcast([P, P]),
                        rhs=vec_rows[:],
                        start=True,
                        stop=True,
                    )
                nc.vector.tensor_copy(
                    out=everywhere[:, 2 * CHUNK * half : 2 * CHUNK * (half + 1)], in_=row_bank[:]
                )

        def products(acts_codes, acts_scales, codes, scales, passes, t):
            acc = psum_acc.tile([P, CHUNK], F32, tag="acc")
            tokens = slice(P * t, P * (t + 1))
            for c in range(passes):
                nc.tensor.matmul_mx(
                    out=acc[:],
                    lhsT=acts_codes[:, c, tokens].bitcast(FP8X4),
                    lhsT_scale=acts_scales[:, c, tokens],
                    rhs=codes[:, c, :].bitcast(FP8X4),
                    rhs_scale=scales[:, c, :],
                    start=(c == 0),
                    stop=(c == passes - 1),
                )
            return acc

        def add_bias(dest, acc, bias):
            nc.vector.tensor_tensor(
                out=dest.rearrange("p (j e) -> p j e", e=ROWS_PER_PARTITION),
                in0=acc[:].rearrange("p (e j) -> p j e", e=ROWS_PER_PARTITION),
                in1=bias.rearrange("p (j e) -> p j e", e=ROWS_PER_PARTITION),
                op=ALU.add,
            )

        def layer1_products(n):
            i = n // PASSES_1
            c = n % PASSES_1
            for t in range(TOKEN_TILES):
                if c == 0:
                    acc = psum_acc.tile([P, CHUNK], F32, tag="acc")
                    acc_tiles[(i, t)] = acc
                nc.tensor.matmul_mx(
                    out=acc_tiles[(i, t)][:],
                    lhsT=u_codes[:, c, P * t : P * (t + 1)].bitcast(FP8X4),
                    lhsT_scale=u_scales[:, c, P * t : P * (t + 1)],
                    rhs=w1_codes[:, i, c, :].bitcast(FP8X4),
                    rhs_scale=w1_scales[:, i, c, :],
                    start=(c == 0),
                    stop=(c == PASSES_1 - 1),
                )
            if c == PASSES_1 - 1:
                for t in range(TOKEN_TILES):
                    h_biased = biased.tile([P, CHUNK], F32, tag="h_biased")
                    add_bias(h_biased[:], acc_tiles[(i, t)], b1_all[:, CHUNK * i : CHUNK * (i + 1)])
                    h_tiles[(i, t)] = h_biased

        def layer1_squares(i):
            for t in range(TOKEN_TILES):
                squares = unread.tile([P, CHUNK], BF16, tag="squares")
                nc.scalar.activation(
                    out=squares[:],
                    in_=h_tiles[(i, t)][:],
                    func=ACT.Square,
                    accum_out=square_sums[:, t, i : i + 1],
                )

        def layer1_gains(i):
            columns = slice(CHUNK * i, CHUNK * (i + 1))
            for t in range(TOKEN_TILES):
                nc.vector.tensor_tensor(
                    out=gained[:, t, columns],
                    in0=h_tiles[(i, t)][:],
                    in1=nw_all[:, columns],
                    op=ALU.mult,
                )

        nc.vector.memset(vec_rows[:], 0.0)
        for first_row, vector in ((0, tok_b1), (ROW_PIECES, tok_nw)):
            nc.sync.dma_start(
                out=vec_rows[first_row : first_row + ROW_PIECES, :],
                in_=vector.rearrange("(r n) -> r n", r=ROW_PIECES),
            )
        u_view = u_sb[:].rearrange("p (t k) -> p t k", t=TOKEN_TILES)
        nc.sync.dma_start(
            out=u_view[:, :, 0:STOCH], in_=stoch.rearrange("(p t) k -> p t k", t=TOKEN_TILES)
        )
        nc.sync.dma_start(
            out=u_view[:, :, STOCH:K1], in_=action.rearrange("(p t) k -> p t k", t=TOKEN_TILES)
        )
        for i in range(RAW_BUFS):
            rawi = raw_pool.tile([P, ROWS_PER_PARTITION * K1], BF16, tag="raw")
            raw_w1[i] = rawi
            for k in range(2):
                nc.sync.dma_start(
                    out=rawi[:].rearrange("j (e k) -> j e k", e=ROWS_PER_PARTITION)[:, 2 * k : 2 * k + 2, :],
                    in_=tok_w1[CHUNK * i : CHUNK * (i + 1), :].rearrange("(j e) k -> j e k", e=ROWS_PER_PARTITION)[:, 2 * k : 2 * k + 2, :])

        make_identity(nc, ident_bf[:])
        make_identity(nc, ident[:])
        nc.vector.memset(minus_half[:], -0.5)
        nc.scalar.activation(out=table_warmer[:], in_=minus_half[:], func=ACT.Silu)


        EN = {'S': nc.scalar.copy, 'V': nc.vector.tensor_copy}
        banks = {}
        grouped = {}
        NW1 = CHUNKS * PASSES_1
        def T(n):
            if n < NW1:
                banks[n] = w1_transposes(n)
            else:
                banks[n] = w2_transposes(n - NW1)
        def C(n, e='SS'):
            g = stage.tile([P, ROWS_PER_PARTITION * P * PACK], BF16, tag="grouped", align_bytes=64)
            grouped[n] = g
            for k in range(2):
                C1(n, k, e[k])
        def CA(n, e):
            g = stage.tile([P, ROWS_PER_PARTITION * P * PACK], BF16, tag="grouped", align_bytes=64)
            grouped[n] = g
            C1(n, 0, e)
        def CB(n, e):
            C1(n, 1, e)
        def C1(n, k, e):
            gw = grouped[n][:].bitcast(F32).rearrange("p (b r h) -> p b r h", b=ROWS_PER_PARTITION, h=2)
            EN[e](out=gw[:, 2 * k : 2 * k + 2], in_=banks[n][k][:].rearrange("p b h r -> p b r h"))
        def Q(n):
            if n < NW1:
                i, c = n // PASSES_1, n % PASSES_1
                co, sc = w1_codes[:, i, c, :], w1_scales[:, i, c, :]
                if c == PASSES_1 - 1:
                    raw_w2[i] = load_chunk(tok_w2, i, 1)
                    if i == 2:
                        nc.sync.dma_start(out=b2_all[:], in_=tok_b2.partition_broadcast(P))
            else:
                i, c = (n - NW1) // PASSES_2, (n - NW1) % PASSES_2
                co, sc = w2_codes[:, i, c, :], w2_scales[:, i, c, :]
            nc.vector.quantize_mx(out=co.bitcast(FP8X4), scales=sc, in_=grouped[n][:])
        def M1(i, ts, cs):
            for t in ts:
                if cs[0] == 0:
                    acc = psum_acc.tile([P, CHUNK], F32, tag="acc")
                    acc_tiles[(i, t)] = acc
                for c in cs:
                    nc.tensor.matmul_mx(
                        out=acc_tiles[(i, t)][:],
                        lhsT=u_codes[:, c, P * t : P * (t + 1)].bitcast(FP8X4),
                        lhsT_scale=u_scales[:, c, P * t : P * (t + 1)],
                        rhs=w1_codes[:, i, c, :].bitcast(FP8X4),
                        rhs_scale=w1_scales[:, i, c, :],
                        start=(c == 0), stop=(c == PASSES_1 - 1))
        def A(i, t):
            h_biased = biased.tile([P, CHUNK], F32, tag="h_biased")
            add_bias(h_biased[:], acc_tiles[(i, t)], b1_all[:, CHUNK * i : CHUNK * (i + 1)])
            h_tiles[(i, t)] = h_biased
        def SQ(i, t):
            squares = unread.tile([P, CHUNK], BF16, tag="squares")
            nc.scalar.activation(out=squares[:], in_=h_tiles[(i, t)][:], func=ACT.Square,
                accum_out=square_sums[:, t, i : i + 1])
        def G(i, t):
            columns = slice(CHUNK * i, CHUNK * (i + 1))
            nc.vector.tensor_tensor(out=gained[:, t, columns], in0=h_tiles[(i, t)][:], in1=nw_all[:, columns], op=ALU.mult)
        def N(t):
            nc.vector.tensor_reduce(out=row_sum[:, t:t+1], in_=square_sums[:, t, :], axis=AXIS.X, op=ALU.add)
            nc.vector.tensor_scalar(out=mean_eps[:, t:t+1], in0=row_sum[:, t:t+1], scalar1=1.0 / HIDDEN, scalar2=EPS, op0=ALU.mult, op1=ALU.add)
            nc.gpsimd.tensor_tensor(out=rstd[:, t:t+1], in0=mean_eps[:, t:t+1], in1=minus_half[:, t:t+1], op=ALU.pow)
        gb = {}
        def U(t, c, w=1):
            nc.scalar.activation(
                out=g_sb[:, HIDDEN * t + K_PASS * c : HIDDEN * t + K_PASS * (c + w)],
                in_=gained[:, t, K_PASS * c : K_PASS * (c + w)],
                func=ACT.Silu, scale=rstd[:, t : t + 1])
        def GT(t, p):
            words = g_sb[:].bitcast(F32)
            bank = psum_t.tile([P, 2, 2, P], F32, tag="bank")
            for k in range(2):
                for h in range(2):
                    first = t * (HIDDEN // 2) + WORDS_PER_PASS * (2 * p + k) + P * h
                    nc.tensor.transpose(bank[:, k, h, :], words[:, first : first + P], ident[:])
            gb[(t, p)] = bank
        def GC(t, p, e='V'):
            g = stage.tile([P, ROWS_PER_PARTITION * P * PACK], BF16, tag="grouped", align_bytes=64)
            grouped[('g', t, p)] = g
            gw = g[:, 0 : 2 * P * PACK].bitcast(F32).rearrange("p (b r h) -> p b r h", b=2, h=2)
            EN[e](out=gw, in_=gb[(t, p)][:].rearrange("p b h r -> p b r h"))
        def GQ(t, p):
            nc.vector.quantize_mx(
                out=g_codes[:, t, 2 * p : 2 * p + 2, :].rearrange("p c n -> p (c n)").bitcast(FP8X4),
                scales=g_scales[:, t, 2 * p : 2 * p + 2, :].rearrange("p c n -> p (c n)"),
                in_=grouped[('g', t, p)][:, 0 : 2 * P * PACK])
        acc2 = {}
        def M2(i, t, cs=(0, 1, 2, 3)):
            if cs[0] == 0:
                acc = psum_acc.tile([P, CHUNK], F32, tag="acc")
                acc2[(i, t)] = acc
            for c in cs:
                nc.tensor.matmul_mx(out=acc2[(i, t)][:],
                    lhsT=g_codes[:, t, c, :].bitcast(FP8X4), lhsT_scale=g_scales[:, t, c, :],
                    rhs=w2_codes[:, i, c, :].bitcast(FP8X4), rhs_scale=w2_scales[:, i, c, :],
                    start=(c == 0), stop=(c == PASSES_2 - 1))
        outv = out.rearrange("(p t) n -> p t n", t=TOKEN_TILES)
        def O(i, t):
            columns = slice(CHUNK * i, CHUNK * (i + 1))
            out_sb = result.tile([P, CHUNK], F32, tag="out_sb")
            add_bias(out_sb[:], acc2[(i, t)], b2_all[:, columns])
            nc.sync.dma_start(out=outv[:, t, columns], in_=out_sb[:])

        def UT(c):
            ub[c] = transposes(u_sb, K1, TOKEN_TILES, c)
        ub = {}
        def UC(c, e):
            g = stage.tile([P, ROWS_PER_PARTITION * P * PACK], BF16, tag="grouped", align_bytes=64)
            grouped[('u', c)] = g
            gw = g[:, 0 : 2 * P * PACK].bitcast(F32).rearrange("p (b r h) -> p b r h", b=2, h=2)
            EN[e](out=gw, in_=ub[c][0][:].rearrange("p b h r -> p b r h"))
        def UQ(c):
            nc.vector.quantize_mx(out=u_codes[:, c, :].bitcast(FP8X4), scales=u_scales[:, c, :], in_=grouped[('u', c)][:, 0 : 2 * P * PACK])
        def CL():
            nc.vector.tensor_scalar(out=u_view[:, :, STOCH:K1], in0=u_view[:, :, STOCH:K1], scalar1=1.0, scalar2=-1.0, op0=ALU.min, op1=ALU.max)
        def SP(v, h):
            spread_vector(v * ROW_PIECES, (b1_all, nw_all, b2_all)[v], (h,))

        g_codes2 = g_codes[:].rearrange("p t c n -> p (t c n)").rearrange("p (c n) -> p c n", c=PASSES_2)
        g_scales2 = g_scales[:].rearrange("p t c n -> p (t c n)").rearrange("p (c n) -> p c n", c=PASSES_2)
        def GT2(c):
            gb[c] = transposes(g_sb, HIDDEN, TOKEN_TILES, c)[0]
        def GC2(c, e='V'):
            g = stage.tile([P, ROWS_PER_PARTITION * P * PACK], BF16, tag="grouped", align_bytes=64)
            grouped[('g', c)] = g
            gw = g[:, 0 : 2 * P * PACK].bitcast(F32).rearrange("p (b r h) -> p b r h", b=2, h=2)
            EN[e](out=gw, in_=gb[c][:].rearrange("p b h r -> p b r h"))
        def GQ2(c):
            nc.vector.quantize_mx(out=g_codes2[:, c, :].bitcast(FP8X4), scales=g_scales2[:, c, :], in_=grouped[('g', c)][:, 0 : 2 * P * PACK])
        def M2(i, ts, cs=(0, 1, 2, 3)):
            for t in ts:
                if cs[0] == 0:
                    acc = psum_acc.tile([P, CHUNK], F32, tag="acc")
                    acc2[(i, t)] = acc
                for c in cs:
                    nc.tensor.matmul_mx(out=acc2[(i, t)][:],
                        lhsT=g_codes2[:, c, P * t : P * (t + 1)].bitcast(FP8X4), lhsT_scale=g_scales2[:, c, P * t : P * (t + 1)],
                        rhs=w2_codes[:, i, c, :].bitcast(FP8X4), rhs_scale=w2_scales[:, i, c, :],
                        start=(c == 0), stop=(c == PASSES_2 - 1))

        def TA(n):
            words = raw_w2[(n - NW1) // PASSES_2][:].bitcast(F32)
            bs = []
            for pair in range(2):
                bank = psum_acc.tile([P, 2, 2, P], F32, tag="acc")
                for b in range(2):
                    for h in range(2):
                        first = (2 * pair + b) * (HIDDEN // 2) + WORDS_PER_PASS * ((n - NW1) % PASSES_2) + P * h
                        nc.tensor.transpose(bank[:, b, h, :], words[:, first : first + P], ident[:])
                bs.append(bank)
            banks[n] = bs

        def GT2(c):
            words = g_sb[:].bitcast(F32)
            bank = psum_acc.tile([P, 2, 2, P], F32, tag="acc")
            for b in range(2):
                for h in range(2):
                    first = b * (HIDDEN // 2) + WORDS_PER_PASS * c + P * h
                    nc.tensor.transpose(bank[:, b, h, :], words[:, first : first + P], ident[:])
            gb[c] = bank

        def SPA(v, half):
            row_bank = psum_acc.tile([P, 2 * CHUNK], BF16, tag="acc")
            for quarter in range(2):
                row = v * ROW_PIECES + 2 * half + quarter
                nc.tensor.matmul(out=row_bank[:, CHUNK * quarter : CHUNK * (quarter + 1)], lhsT=ident_bf[:, row : row + 1].to_broadcast([P, P]), rhs=vec_rows[:], start=True, stop=True)
            EN['S'](out=b2_all[:, 2 * CHUNK * half : 2 * CHUNK * (half + 1)], in_=row_bank[:])

        def MP(n):
            i, c = n // PASSES_1, n % PASSES_1
            M1(i, (0, 1), (c,))

        def MP2(m):
            M2(m // PASSES_2, (0, 1), (m % PASSES_2,))

        def NB():
            nc.vector.tensor_reduce(out=row_sum[:], in_=square_sums[:], axis=AXIS.X, op=ALU.add)
            nc.vector.tensor_scalar(out=mean_eps[:], in0=row_sum[:], scalar1=1.0 / HIDDEN, scalar2=EPS, op0=ALU.mult, op1=ALU.add)
            nc.gpsimd.tensor_tensor(out=rstd[:], in0=mean_eps[:], in1=minus_half[:], op=ALU.pow)

        def SA(v, half):
            row_bank = psum_acc.tile([P, 2 * CHUNK], BF16, tag="acc")
            for quarter in range(2):
                row = v * ROW_PIECES + 2 * half + quarter
                nc.tensor.matmul(out=row_bank[:, CHUNK * quarter : CHUNK * (quarter + 1)], lhsT=ident_bf[:, row : row + 1].to_broadcast([P, P]), rhs=vec_rows[:], start=True, stop=True)
            nc.vector.tensor_copy(out=(b1_all, nw_all, b2_all)[v][:, 2 * CHUNK * half : 2 * CHUNK * (half + 1)], in_=row_bank[:])

        def DM(c, k):
            bank = psum_acc.tile([P, 2, 2, P], F32, tag="acc")
            gb[c] = bank
            for _ in range(k):
                nc.tensor.matmul(out=bank[:].rearrange("p b h r -> p (b h r)"), lhsT=ident_bf[:], rhs=vec_rows[:], start=True, stop=True)
        def GT2(c):
            words = g_sb[:].bitcast(F32)
            if c not in gb:
                bank = psum_acc.tile([P, 2, 2, P], F32, tag="acc")
                gb[c] = bank
            for b in range(2):
                for h in range(2):
                    first = b * (HIDDEN // 2) + WORDS_PER_PASS * c + P * h
                    nc.tensor.transpose(gb[c][:, b, h, :], words[:, first : first + P], ident[:])

        def TB(n, k):
            words = raw_w2[(n - NW1) // PASSES_2][:].bitcast(F32)
            bank = psum_t.tile([P, 2, 2, P], F32, tag="bank")
            for b in range(2):
                for h in range(2):
                    first = (2 * k + b) * (HIDDEN // 2) + WORDS_PER_PASS * ((n - NW1) % PASSES_2) + P * h
                    nc.tensor.transpose(bank[:, b, h, :], words[:, first : first + P], ident[:])
            banks.setdefault(n, []).append(bank)
        def X(a, b):
            for k in range(a, b):
                i, c, t = k // 8, k % 8 // 2, k % 2
                M2(i, (t,), (c,))

        def ML(ts, cs):
            for c in cs:
                for t in ts:
                    if c == 0:
                        acc = psum_t.tile([P, CHUNK], F32, tag="bank")
                        acc2[(3, t)] = acc
                    nc.tensor.matmul_mx(out=acc2[(3, t)][:],
                        lhsT=g_codes2[:, c, P * t : P * (t + 1)].bitcast(FP8X4), lhsT_scale=g_scales2[:, c, P * t : P * (t + 1)],
                        rhs=w2_codes[:, 3, c, :].bitcast(FP8X4), rhs_scale=w2_scales[:, 3, c, :],
                        start=(c == 0), stop=(c == PASSES_2 - 1))

        def DX(c, k):
            if c not in gb:
                bank = psum_acc.tile([P, 2, 2, P], F32, tag="acc")
                gb[c] = bank
            for _ in range(k):
                nc.tensor.matmul(out=gb[c][:].rearrange("p b h r -> p (b h r)"), lhsT=ident_bf[:], rhs=vec_rows[:], start=True, stop=True)

        def D1(k):
            idle = psum_acc.tile([P, CHUNK], F32, tag="acc")
            for _ in range(k):
                nc.tensor.matmul(out=idle[:], lhsT=ident_bf[:], rhs=vec_rows[:], start=True, stop=True)

        def NA(t):
            nc.vector.tensor_scalar(out=scaled[:, t, :], in0=square_sums[:, t, :], scalar1=1.0 / HIDDEN, scalar2=EPS, op0=ALU.mult, op1=ALU.add, accum_out=mean_eps[:, t : t + 1])
        def NP():
            nc.gpsimd.tensor_tensor(out=rstd[:], in0=mean_eps[:], in1=minus_half[:], op=ALU.pow)
        scaled = keep.tile([P, TOKEN_TILES, CHUNKS], F32)

        def H(m):
            i, k, c = m // 6, m % 6 // 3, m % 3
            n = 3 * i + c
            words = raw_w1[i][:].bitcast(F32)
            bank = psum_t.tile([P, 2, 2, P], F32, tag="bank")
            for b in range(2):
                for h in range(2):
                    first = (2 * k + b) * (K1 // 2) + WORDS_PER_PASS * c + P * h
                    nc.tensor.transpose(bank[:, b, h, :], words[:, first : first + P], ident[:])
            banks.setdefault(n, []).append(bank)
        def HC(m, e='S'):
            i, k, c = m // 6, m % 6 // 3, m % 3
            n = 3 * i + c
            if k == 0:
                g = stage.tile([P, ROWS_PER_PARTITION * P * PACK], BF16, tag="grouped", align_bytes=64)
                grouped[n] = g
            C1(n, k, e)
        def H3(i, k):
            for c in range(3):
                H(6 * i + 3 * k + c)
        def C3(i, k, e='SSS'):
            for c in range(3):
                HC(6 * i + 3 * k + c, e[c])


        SA(0, 0); SA(0, 1)
        UT(0); UC(0, 'S')
        UT(1); UC(1, 'S')
        SA(1, 0)
        H3(0, 0)
        UQ(0)
        CL()
        UQ(1)
        SA(1, 1)
        C3(0, 0)
        H3(0, 1)
        C3(0, 1)
        UT(2)
        Q(0)
        UC(2, 'S')
        D1(1)
        H3(1, 0)
        D1(2)
        Q(1)
        UQ(2)
        Q(2)
        C3(1, 0, 'SSV')
        H3(1, 1)
        M1(0, (0,), (0, 1, 2))
        C3(1, 1)
        Q(3)
        A(0, 0)
        Q(4)
        H3(2, 0)
        M1(0, (1,), (0, 1, 2))
        Q(5)
        A(0, 1)
        C3(2, 0)
        SQ(0, 0)
        G(0, 0)
        H3(2, 1)
        M1(1, (0,), (0, 1, 2))
        G(0, 1)
        C3(2, 1)
        SQ(0, 1)
        A(1, 0)
        Q(6); Q(7)
        H3(3, 0)
        M1(1, (1,), (0, 1, 2))
        C3(3, 0)
        Q(8)
        A(1, 1)
        H3(3, 1)
        M1(2, (0,), (0, 1, 2))
        G(1, 0)
        C3(3, 1)
        A(2, 0)
        Q(9)
        SQ(1, 0)
        SQ(1, 1)
        M1(2, (1,), (0, 1, 2))
        T(12)
        Q(10)
        SQ(2, 0)
        A(2, 1)

        M1(3, (0, 1), (0, 1))
        C(12)
        SQ(2, 1)
        Q(11)
        M1(3, (0, 1), (2,))
        T(13)
        G(1, 1)
        A(3, 0); A(3, 1)
        CA(13, 'S')
        SQ(3, 0); SQ(3, 1)
        CB(13, 'S')
        T(14); T(15)
        DX(0, 2)
        T(16)
        G(2, 0)
        G(2, 1)
        NB()
        C(14, 'VV')
        T(17)
        C(15, 'SS')
        CA(16, 'S')
        T(18)
        U(0, 0); U(1, 0)
        G(3, 0); G(3, 1)
        U(0, 1); U(1, 1)
        Q(12)
        Q(13)
        DX(0, 1)
        GT2(0)
        GC2(0, 'V')
        Q(14)
        GQ2(0)
        U(0, 2); U(1, 2)
        DX(1, 2)
        GT2(1)
        GC2(1, 'V')
        Q(15)
        GQ2(1)
        U(0, 3); U(1, 3)
        DX(2, 2)
        GT2(2)
        GC2(2, 'S')
        DX(3, 1)
        GT2(3)
        GC2(3, 'S')
        GQ2(2)
        GQ2(3)
        M2(0, (0,), (0, 1, 2))
        CB(16, 'S')
        C(17, 'SS')
        Q(16)
        M2(0, (1,), (0, 1, 2))
        M2(0, (0, 1), (3,))
        T(19)
        C(18)
        O(0, 0)
        Q(17)
        O(0, 1)
        T(20)
        C(19)
        Q(18)
        M2(1, (0, 1), (0, 1))
        Q(19)
        T(21); T(22)
        C(20)
        Q(20)
        C(21)
        M2(1, (0, 1), (2, 3))
        Q(21)
        T(23); T(24)
        C(22)
        O(1, 0); O(1, 1)
        Q(22)
        M2(2, (0, 1), (0, 1))
        C(23); Q(23)
        T(25); T(26)
        C(24, 'SS')
        Q(24)
        M2(2, (0, 1), (2, 3))
        C(25); Q(25)
        T(27)
        C(26, 'SS')
        O(2, 0)
        Q(26)
        C(27, 'SS')
        O(2, 1)
        ML((0, 1), (0, 1, 2))
        Q(27)
        ML((0, 1), (3,))
        O(3, 0); O(3, 1)
